import numpy as np
import ml_dtypes


def mxq(x, axis, fmt="e4m3"):
    dtype, down = {"e4m3": (ml_dtypes.float8_e4m3fn, 7), "e5m2": (ml_dtypes.float8_e5m2, 14)}[fmt]
    v = np.moveaxis(np.asarray(x, np.float32).astype(ml_dtypes.bfloat16).astype(np.float64), axis, -1)
    blocks = v.reshape(v.shape[:-1] + (-1, 32))
    amax = np.abs(blocks).max(-1, keepdims=True)
    byte = np.maximum(np.where(amax > 0, np.frexp(amax)[1] - 1 + 127, 0) - down, 1)
    scale = np.exp2(byte - 127.0)
    codes = (blocks / scale).astype(np.float32).astype(dtype).astype(np.float64)
    return np.moveaxis((codes * scale).reshape(v.shape), -1, axis)


WIDE = False


def mx_kscale(k):
    if not WIDE:
        return np.ones(k)
    levels = np.array([10, -10, 5, -5, 0])
    a = np.random.permutation(np.resize(levels, k // 512 * 4)).reshape(k // 512, 4)
    idx = np.arange(k)
    return np.exp2(a[idx // 512, idx % 128 // 32])


BF16 = ml_dtypes.bfloat16


def bf(x):
    return np.asarray(x, np.float32).astype(BF16)


def f64(x):
    return np.asarray(x).astype(np.float64)


B, N, F_IN, F_OUT, K = 32, 512, 128, 128, 4
KF = K * F_IN


def setup_inputs():
    s = mx_kscale(N)
    r = (s.min() / s)[:, None]
    u = mx_kscale(KF)[:F_IN]

    def term(g):
        return bf(np.random.standard_normal((B, N, F_IN)) * g * r * u)

    return {"x": term(1.0), "x1": term(0.7), "x2": term(0.7), "xt2": term(1.0),
            "L": bf(np.random.standard_normal((N, N)) * 0.7 / np.sqrt(N) * s[None, :] / s[:, None]),
            "weight": bf(np.random.standard_normal((K, F_IN, F_OUT)) / np.sqrt(KF) / u[None, :, None]),
            "bias": bf(np.random.standard_normal((1, N, F_OUT)) * 0.3 * r)}


def reference(x, x1, x2, xt2, L, weight, bias):
    x3 = mxq(f64(L), 1, "e4m3") @ mxq(f64(x2), 1, "e4m3")
    xt3 = 2.0 * x3 - f64(x1)
    xc = np.concatenate([f64(x), f64(x1), f64(xt2), xt3], axis=2)
    return (mxq(xc, 2, "e4m3") @ mxq(f64(weight).reshape(KF, F_OUT), 0, "e4m3")) + f64(bias)

@@ -1,0 +1,209 @@
+from contextlib import ExitStack
+
+import concourse.mybir as mybir
+from concourse.masks import make_identity
+
+BF16 = mybir.dt.bfloat16
+F32 = mybir.dt.float32
+U32 = mybir.dt.uint32
+U8 = mybir.dt.uint8
+FP8X4 = mybir.dt.float8_e4m3fn_x4
+ALU = mybir.AluOpType
+
+P = 128
+PACK = 4
+BATCH = 32
+NODES = 512
+FEAT = 128
+ORDERS = 4
+ROWS = NODES // P
+GROUP = 4
+N_GROUPS = BATCH // GROUP
+LOAD_BUFS = 6
+LOAD_AHEAD = LOAD_BUFS - 1
+LAG = 2
+
+FLOPS = 2 * BATCH * NODES * NODES * FEAT + 2 * BATCH * NODES * ORDERS * FEAT * FEAT
+
+
+def tile_gcncheb_pb_t_kernel(tc, x, x1, x2, xt2, L, weight, bias, out):
+    nc = tc.nc
+    with ExitStack() as ctx:
+        const = ctx.enter_context(tc.tile_pool(name="const", bufs=1))
+        loads = ctx.enter_context(tc.tile_pool(name="loads", bufs=LOAD_BUFS))
+        per_group = ctx.enter_context(tc.tile_pool(name="per_group", bufs=2))
+        per_item = ctx.enter_context(tc.tile_pool(name="per_item", bufs=LAG + 2))
+        stores = ctx.enter_context(tc.tile_pool(name="stores", bufs=3))
+        psum_x3 = ctx.enter_context(tc.psum_pool(name="psum_x3", bufs=2))
+        psum_t = ctx.enter_context(tc.psum_pool(name="psum_t", bufs=4))
+        psum_out = ctx.enter_context(tc.psum_pool(name="psum_out", bufs=2))
+
+        def load_group(src, g, name):
+            rows = loads.tile([P, GROUP, ROWS, FEAT], BF16, name=name)
+            nc.sync.dma_start(
+                out=rows[:],
+                in_=src[g * GROUP : (g + 1) * GROUP].rearrange("c (r i) f -> r c i f", i=ROWS),
+            )
+            return rows
+
+        l_rows = const.tile([P, ROWS, NODES], BF16)
+        nc.sync.dma_start(out=l_rows[:], in_=L.rearrange("(r i) m -> r i m", i=ROWS))
+        inputs = {}
+
+        def load_inputs(g):
+            inputs[g] = {
+                "x2": load_group(x2, g, "x2_rows"),
+                "x1": load_group(x1, g, "x1_rows"),
+                "x": load_group(x, g, "x_rows"),
+                "xt2": load_group(xt2, g, "xt2_rows"),
+            }
+
+        load_inputs(0)
+        w_rows = const.tile([P, ORDERS, FEAT], BF16)
+        nc.sync.dma_start(out=w_rows[:], in_=weight.rearrange("t f o -> f t o"))
+        bias_rows = const.tile([P, ROWS * FEAT], BF16)
+        nc.sync.dma_start(out=bias_rows[:], in_=bias[0].rearrange("(r i) o -> r (i o)", i=ROWS))
+        for g in range(1, LOAD_AHEAD):
+            load_inputs(g)
+
+        ident = const.tile([P, P], BF16)
+        make_identity(nc, ident[:])
+
+        l_grouped = const.tile([P, ROWS, P, PACK], BF16, align_bytes=64)
+        for half in range(ROWS // 2):
+            l_planes = psum_t.tile([P, 2, PACK, P], BF16, name="planes")
+            for i2 in range(2):
+                l_cols = l_rows[:, 2 * half + i2, :].rearrange("r (p t) -> r p t", t=PACK)
+                for t in range(PACK):
+                    nc.tensor.transpose(l_planes[:, i2, t, :], l_cols[:, :, t], ident[:])
+            nc.scalar.copy(
+                out=l_grouped[:, 2 * half : 2 * half + 2],
+                in_=l_planes[:].rearrange("p i t r -> p i r t"),
+            )
+        l_codes = const.tile([P, ROWS * P], U32, align_bytes=64)
+        l_scales = const.tile([P, ROWS * P], U8, align_bytes=64)
+        nc.vector.quantize_mx(
+            out=l_codes[:].bitcast(FP8X4),
+            scales=l_scales[:],
+            in_=l_grouped[:].rearrange("p i r t -> p (i r t)"),
+        )
+
+        w_grouped = const.tile([P, FEAT, ORDERS], BF16, align_bytes=64)
+        nc.vector.tensor_copy(out=w_grouped[:], in_=w_rows[:].rearrange("f t o -> f o t"))
+        w_codes = const.tile([P, FEAT], U32, align_bytes=64)
+        w_scales = const.tile([P, FEAT], U8, align_bytes=64)
+        nc.vector.quantize_mx(
+            out=w_codes[:].bitcast(FP8X4),
+            scales=w_scales[:],
+            in_=w_grouped[:].rearrange("f o t -> f (o t)"),
+        )
+
+        x2_quantised = {}
+        xt3_rows = {}
+        xc_quantised = {}
+        out_rows = {}
+
+        def quantise_x2(g):
+            x2_grouped = per_group.tile([P, GROUP, FEAT, PACK], BF16, align_bytes=64)
+            nc.vector.tensor_copy(
+                out=x2_grouped[:], in_=inputs[g]["x2"][:].rearrange("p c j f -> p c f j")
+            )
+            x2_codes = per_group.tile([P, GROUP * FEAT], U32, align_bytes=64)
+            x2_scales = per_group.tile([P, GROUP * FEAT], U8, align_bytes=64)
+            nc.vector.quantize_mx(
+                out=x2_codes[:].bitcast(FP8X4),
+                scales=x2_scales[:],
+                in_=x2_grouped[:].rearrange("p c f j -> p (c f j)"),
+            )
+            x2_quantised[g] = (x2_codes, x2_scales)
+            xt3_rows[g] = per_group.tile([P, GROUP, ROWS, FEAT], BF16, name="xt3_rows")
+
+        def recurrence(g, i):
+            x2_codes, x2_scales = x2_quantised[g]
+            node_cols = slice(i * P, (i + 1) * P)
+            x3 = psum_x3.tile([P, GROUP * FEAT], F32)
+            nc.tensor.matmul_mx(
+                out=x3[:],
+                lhsT=l_codes[:, node_cols].bitcast(FP8X4),
+                lhsT_scale=l_scales[:, node_cols],
+                rhs=x2_codes[:].bitcast(FP8X4),
+                rhs_scale=x2_scales[:],
+                start=True,
+                stop=True,
+            )
+            nc.vector.scalar_tensor_tensor(
+                out=xt3_rows[g][:, :, i, :],
+                in0=x3[:].rearrange("r (c f) -> r c f", f=FEAT),
+                scalar=2.0,
+                in1=inputs[g]["x1"][:, :, i, :],
+                op0=ALU.mult,
+                op1=ALU.subtract,
+            )
+
+        def transpose_item(c):
+            g, k = divmod(c, GROUP)
+            orders = (inputs[g]["x"], inputs[g]["x1"], inputs[g]["xt2"], xt3_rows[g])
+            xc_grouped = per_item.tile([P, ROWS, P, ORDERS], BF16, align_bytes=64)
+            for half in range(ROWS // 2):
+                planes = psum_t.tile([P, 2, ORDERS, P], BF16)
+                for i2 in range(2):
+                    for t in range(ORDERS):
+                        nc.tensor.transpose(
+                            planes[:, i2, t, :], orders[t][:, k, 2 * half + i2, :], ident[:]
+                        )
+                nc.scalar.copy(
+                    out=xc_grouped[:, 2 * half : 2 * half + 2],
+                    in_=planes[:].rearrange("f i t r -> f i r t"),
+                )
+            return xc_grouped
+
+        def quantise_item(c, xc_grouped):
+            xc_codes = per_item.tile([P, ROWS * P], U32, align_bytes=64)
+            xc_scales = per_item.tile([P, ROWS * P], U8, align_bytes=64)
+            nc.vector.quantize_mx(
+                out=xc_codes[:].bitcast(FP8X4),
+                scales=xc_scales[:],
+                in_=xc_grouped[:].rearrange("f i r t -> f (i r t)"),
+            )
+            xc_quantised[c] = (xc_codes, xc_scales)
+
+        def filter_item(c):
+            g, k = divmod(c, GROUP)
+            xc_codes, xc_scales = xc_quantised[c]
+            if k == 0:
+                out_rows[g] = stores.tile([P, GROUP, ROWS * FEAT], F32, name="out_rows")
+            acc = psum_out.tile([P, ROWS * FEAT], F32)
+            for i in range(ROWS):
+                node_cols = slice(i * P, (i + 1) * P)
+                nc.tensor.matmul_mx(
+                    out=acc[:, i * FEAT : (i + 1) * FEAT],
+                    lhsT=xc_codes[:, node_cols].bitcast(FP8X4),
+                    lhsT_scale=xc_scales[:, node_cols],
+                    rhs=w_codes[:].bitcast(FP8X4),
+                    rhs_scale=w_scales[:],
+                    start=True,
+                    stop=True,
+                )
+            nc.vector.tensor_tensor(out=out_rows[g][:, k, :], in0=acc[:], in1=bias_rows[:], op=ALU.add)
+            if k == GROUP - 1:
+                nc.gpsimd.dma_start(
+                    out=out[g * GROUP : (g + 1) * GROUP].rearrange("c (r i) o -> r c (i o)", i=ROWS),
+                    in_=out_rows[g][:],
+                )
+
+        quantise_x2(0)
+        for i in range(ROWS):
+            recurrence(0, i)
+        for c in range(BATCH + LAG):
+            g, k = divmod(c, GROUP)
+            if c < BATCH:
+                if k == 0 and g + LOAD_AHEAD < N_GROUPS:
+                    load_inputs(g + LOAD_AHEAD)
+                if k == 0 and g + 1 < N_GROUPS:
+                    quantise_x2(g + 1)
+                xc_grouped = transpose_item(c)
+                if g + 1 < N_GROUPS:
+                    recurrence(g + 1, k)
+                quantise_item(c, xc_grouped)
+            if c >= LAG:
+                filter_item(c - LAG)

@@ -11,12 +11,14 @@ FP8X4 = mybir.dt.float8_e4m3fn_x4
 ALU = mybir.AluOpType
 
 P = 128
+HALF = P // 2
 PACK = 4
 BATCH = 32
 NODES = 512
 FEAT = 128
 ORDERS = 4
 ROWS = NODES // P
+PAIRS = ROWS // 2
 GROUP = 4
 N_GROUPS = BATCH // GROUP
 LOAD_BUFS = 6
@@ -33,9 +35,8 @@ def tile_gcncheb_pb_t_kernel(tc, x, x1, x2, xt2, L, weight, bias, out):
         loads = ctx.enter_context(tc.tile_pool(name="loads", bufs=LOAD_BUFS))
         per_group = ctx.enter_context(tc.tile_pool(name="per_group", bufs=2))
         per_item = ctx.enter_context(tc.tile_pool(name="per_item", bufs=LAG + 2))
-        stores = ctx.enter_context(tc.tile_pool(name="stores", bufs=3))
         psum_x3 = ctx.enter_context(tc.psum_pool(name="psum_x3", bufs=2))
-        psum_t = ctx.enter_context(tc.psum_pool(name="psum_t", bufs=4))
+        psum_t = ctx.enter_context(tc.psum_pool(name="psum_t", bufs=2))
         psum_out = ctx.enter_context(tc.psum_pool(name="psum_out", bufs=2))
 
         def load_group(src, g, name):
@@ -46,8 +47,6 @@ def tile_gcncheb_pb_t_kernel(tc, x, x1, x2, xt2, L, weight, bias, out):
             )
             return rows
 
-        l_rows = const.tile([P, ROWS, NODES], BF16)
-        nc.sync.dma_start(out=l_rows[:], in_=L.rearrange("(r i) m -> r i m", i=ROWS))
         inputs = {}
 
         def load_inputs(g):
@@ -58,26 +57,34 @@ def tile_gcncheb_pb_t_kernel(tc, x, x1, x2, xt2, L, weight, bias, out):
                 "xt2": load_group(xt2, g, "xt2_rows"),
             }
 
+        l_rows = const.tile([P, ROWS, NODES], BF16)
+        nc.sync.dma_start(out=l_rows[:], in_=L.rearrange("(r i) m -> r i m", i=ROWS))
         load_inputs(0)
-        w_rows = const.tile([P, ORDERS, FEAT], BF16)
-        nc.sync.dma_start(out=w_rows[:], in_=weight.rearrange("t f o -> f t o"))
+        w_rows = const.tile([P, ORDERS, 2, FEAT], BF16)
+        for h in range(2):
+            nc.sync.dma_start(
+                out=w_rows[h * HALF : (h + 1) * HALF],
+                in_=weight.rearrange("j (w e) o -> w j e o", e=2),
+            )
         bias_rows = const.tile([P, ROWS * FEAT], BF16)
         nc.sync.dma_start(out=bias_rows[:], in_=bias[0].rearrange("(r i) o -> r (i o)", i=ROWS))
         for g in range(1, LOAD_AHEAD):
             load_inputs(g)
 
-        ident = const.tile([P, P], BF16)
-        make_identity(nc, ident[:])
+        ident_bf16 = const.tile([P, P], BF16)
+        make_identity(nc, ident_bf16[:])
+        ident_f32 = const.tile([P, P], F32)
+        make_identity(nc, ident_f32[:])
 
         l_grouped = const.tile([P, ROWS, P, PACK], BF16, align_bytes=64)
-        for half in range(ROWS // 2):
+        for ip in range(PAIRS):
             l_planes = psum_t.tile([P, 2, PACK, P], BF16, name="planes")
             for i2 in range(2):
-                l_cols = l_rows[:, 2 * half + i2, :].rearrange("r (p t) -> r p t", t=PACK)
+                l_cols = l_rows[:, 2 * ip + i2, :].rearrange("r (p t) -> r p t", t=PACK)
                 for t in range(PACK):
-                    nc.tensor.transpose(l_planes[:, i2, t, :], l_cols[:, :, t], ident[:])
+                    nc.tensor.transpose(l_planes[:, i2, t, :], l_cols[:, :, t], ident_bf16[:])
             nc.scalar.copy(
-                out=l_grouped[:, 2 * half : 2 * half + 2],
+                out=l_grouped[:, 2 * ip : 2 * ip + 2],
                 in_=l_planes[:].rearrange("p i t r -> p i r t"),
             )
         l_codes = const.tile([P, ROWS * P], U32, align_bytes=64)
@@ -88,25 +95,35 @@ def tile_gcncheb_pb_t_kernel(tc, x, x1, x2, xt2, L, weight, bias, out):
             in_=l_grouped[:].rearrange("p i r t -> p (i r t)"),
         )
 
-        w_grouped = const.tile([P, FEAT, ORDERS], BF16, align_bytes=64)
-        nc.vector.tensor_copy(out=w_grouped[:], in_=w_rows[:].rearrange("f t o -> f o t"))
-        w_codes = const.tile([P, FEAT], U32, align_bytes=64)
-        w_scales = const.tile([P, FEAT], U8, align_bytes=64)
+        w_grouped = const.tile([P, 2, 2, FEAT, PACK], BF16, align_bytes=64)
+        nc.vector.memset(w_grouped[:], 0.0)
+        for h in range(2):
+            half = slice(h * HALF, (h + 1) * HALF)
+            for s in range(2):
+                nc.vector.tensor_copy(
+                    out=w_grouped[half, s, h].rearrange("q o (u e) -> q o u e", u=2),
+                    in_=w_rows[half, 2 * s : 2 * s + 2].rearrange("q u e o -> q o u e"),
+                )
+        w_codes = const.tile([P, 2 * 2 * FEAT], U32, align_bytes=64)
+        w_scales = const.tile([P, 2 * 2 * FEAT], U8, align_bytes=64)
         nc.vector.quantize_mx(
             out=w_codes[:].bitcast(FP8X4),
             scales=w_scales[:],
-            in_=w_grouped[:].rearrange("f o t -> f (o t)"),
+            in_=w_grouped[:].rearrange("q s i o t -> q (s i o t)"),
         )
 
         x2_quantised = {}
         xt3_rows = {}
         xc_quantised = {}
-        out_rows = {}
 
         def quantise_x2(g):
+            x2_rows = inputs[g]["x2"]
             x2_grouped = per_group.tile([P, GROUP, FEAT, PACK], BF16, align_bytes=64)
             nc.vector.tensor_copy(
-                out=x2_grouped[:], in_=inputs[g]["x2"][:].rearrange("p c j f -> p c f j")
+                out=x2_grouped[:, 0:2], in_=x2_rows[:, 0:2].rearrange("p c j f -> p c f j")
+            )
+            nc.scalar.copy(
+                out=x2_grouped[:, 2:4], in_=x2_rows[:, 2:4].rearrange("p c j f -> p c f j")
             )
             x2_codes = per_group.tile([P, GROUP * FEAT], U32, align_bytes=64)
             x2_scales = per_group.tile([P, GROUP * FEAT], U8, align_bytes=64)
@@ -142,54 +159,59 @@ def tile_gcncheb_pb_t_kernel(tc, x, x1, x2, xt2, L, weight, bias, out):
 
         def transpose_item(c):
             g, k = divmod(c, GROUP)
-            orders = (inputs[g]["x"], inputs[g]["x1"], inputs[g]["xt2"], xt3_rows[g])
-            xc_grouped = per_item.tile([P, ROWS, P, ORDERS], BF16, align_bytes=64)
-            for half in range(ROWS // 2):
-                planes = psum_t.tile([P, 2, ORDERS, P], BF16)
-                for i2 in range(2):
-                    for t in range(ORDERS):
-                        nc.tensor.transpose(
-                            planes[:, i2, t, :], orders[t][:, k, 2 * half + i2, :], ident[:]
-                        )
-                nc.scalar.copy(
-                    out=xc_grouped[:, 2 * half : 2 * half + 2],
-                    in_=planes[:].rearrange("f i t r -> f i r t"),
-                )
+            xc_grouped = per_item.tile([P, 2 * PAIRS * P * PACK], BF16, align_bytes=64)
+            part = PAIRS * P * PACK
+
+            words = psum_t.tile([P, PAIRS, 2, P], F32)
+            for ip in range(PAIRS):
+                first_word = (k * ROWS + 2 * ip) * (FEAT // 2)
+                for u, name in enumerate(("x", "x1")):
+                    all_words = inputs[g][name][:].rearrange("r c i f -> r (c i f)").bitcast(F32)
+                    nc.tensor.transpose(
+                        words[:, ip, u, :], all_words[:, first_word : first_word + P], ident_f32[:]
+                    )
+            nc.scalar.copy(
+                out=xc_grouped[:, 0:part].bitcast(F32).rearrange("q (ip r u) -> q ip r u", ip=PAIRS, u=2),
+                in_=words[:].rearrange("q ip u r -> q ip r u"),
+            )
+
+            planes = psum_t.tile([P, PAIRS, PACK, P], BF16)
+            for ip in range(PAIRS):
+                for u, rows in enumerate((inputs[g]["xt2"], xt3_rows[g])):
+                    pair = rows[:, k, 2 * ip : 2 * ip + 2, :].rearrange("r i (w e) -> r (i w) e", e=2)
+                    for e in range(2):
+                        nc.tensor.transpose(planes[:, ip, 2 * u + e, :], pair[:, :, e], ident_bf16[:])
+            nc.scalar.copy(
+                out=xc_grouped[:, part : 2 * part].rearrange("q (ip r t) -> q ip r t", ip=PAIRS, t=PACK),
+                in_=planes[:].rearrange("q ip t r -> q ip r t"),
+            )
             return xc_grouped
 
         def quantise_item(c, xc_grouped):
-            xc_codes = per_item.tile([P, ROWS * P], U32, align_bytes=64)
-            xc_scales = per_item.tile([P, ROWS * P], U8, align_bytes=64)
-            nc.vector.quantize_mx(
-                out=xc_codes[:].bitcast(FP8X4),
-                scales=xc_scales[:],
-                in_=xc_grouped[:].rearrange("f i r t -> f (i r t)"),
-            )
+            xc_codes = per_item.tile([P, 2 * PAIRS * P], U32, align_bytes=64)
+            xc_scales = per_item.tile([P, 2 * PAIRS * P], U8, align_bytes=64)
+            nc.vector.quantize_mx(out=xc_codes[:].bitcast(FP8X4), scales=xc_scales[:], in_=xc_grouped[:])
             xc_quantised[c] = (xc_codes, xc_scales)
 
         def filter_item(c):
-            g, k = divmod(c, GROUP)
             xc_codes, xc_scales = xc_quantised[c]
-            if k == 0:
-                out_rows[g] = stores.tile([P, GROUP, ROWS * FEAT], F32, name="out_rows")
             acc = psum_out.tile([P, ROWS * FEAT], F32)
-            for i in range(ROWS):
-                node_cols = slice(i * P, (i + 1) * P)
-                nc.tensor.matmul_mx(
-                    out=acc[:, i * FEAT : (i + 1) * FEAT],
-                    lhsT=xc_codes[:, node_cols].bitcast(FP8X4),
-                    lhsT_scale=xc_scales[:, node_cols],
-                    rhs=w_codes[:].bitcast(FP8X4),
-                    rhs_scale=w_scales[:],
-                    start=True,
-                    stop=True,
-                )
-            nc.vector.tensor_tensor(out=out_rows[g][:, k, :], in0=acc[:], in1=bias_rows[:], op=ALU.add)
-            if k == GROUP - 1:
-                nc.gpsimd.dma_start(
-                    out=out[g * GROUP : (g + 1) * GROUP].rearrange("c (r i) o -> r c (i o)", i=ROWS),
-                    in_=out_rows[g][:],
-                )
+            for ip in range(PAIRS):
+                for s in range(2):
+                    node_cols = slice((s * PAIRS + ip) * P, (s * PAIRS + ip + 1) * P)
+                    w_cols = slice(s * 2 * FEAT, (s + 1) * 2 * FEAT)
+                    nc.tensor.matmul_mx(
+                        out=acc[:, ip * 2 * FEAT : (ip + 1) * 2 * FEAT],
+                        lhsT=xc_codes[:, node_cols].bitcast(FP8X4),
+                        lhsT_scale=xc_scales[:, node_cols],
+                        rhs=w_codes[:, w_cols].bitcast(FP8X4),
+                        rhs_scale=w_scales[:, w_cols],
+                        start=(s == 0),
+                        stop=(s == 1),
+                    )
+            out_rows = per_item.tile([P, ROWS * FEAT], F32)
+            nc.vector.tensor_tensor(out=out_rows[:], in0=acc[:], in1=bias_rows[:], op=ALU.add)
+            nc.gpsimd.dma_start(out=out[c].rearrange("(r i) o -> r (i o)", i=ROWS), in_=out_rows[:])
 
         quantise_x2(0)
         for i in range(ROWS):

@@ -36,7 +36,7 @@ def tile_gcncheb_pb_t_kernel(tc, x, x1, x2, xt2, L, weight, bias, out):
         per_group = ctx.enter_context(tc.tile_pool(name="per_group", bufs=2))
         per_item = ctx.enter_context(tc.tile_pool(name="per_item", bufs=LAG + 2))
         psum_x3 = ctx.enter_context(tc.psum_pool(name="psum_x3", bufs=2))
-        psum_t = ctx.enter_context(tc.psum_pool(name="psum_t", bufs=2))
+        psum_t = ctx.enter_context(tc.psum_pool(name="psum_t", bufs=4))
         psum_out = ctx.enter_context(tc.psum_pool(name="psum_out", bufs=2))
 
         def load_group(src, g, name):
@@ -78,7 +78,7 @@ def tile_gcncheb_pb_t_kernel(tc, x, x1, x2, xt2, L, weight, bias, out):
 
         l_grouped = const.tile([P, ROWS, P, PACK], BF16, align_bytes=64)
         for ip in range(PAIRS):
-            l_planes = psum_t.tile([P, 2, PACK, P], BF16, name="planes")
+            l_planes = psum_t.tile([P, 2, PACK, P], BF16, name="turned")
             for i2 in range(2):
                 l_cols = l_rows[:, 2 * ip + i2, :].rearrange("r (p t) -> r p t", t=PACK)
                 for t in range(PACK):
@@ -162,29 +162,23 @@ def tile_gcncheb_pb_t_kernel(tc, x, x1, x2, xt2, L, weight, bias, out):
             xc_grouped = per_item.tile([P, 2 * PAIRS * P * PACK], BF16, align_bytes=64)
             part = PAIRS * P * PACK
 
-            words = psum_t.tile([P, PAIRS, 2, P], F32)
-            for ip in range(PAIRS):
-                first_word = (k * ROWS + 2 * ip) * (FEAT // 2)
-                for u, name in enumerate(("x", "x1")):
-                    all_words = inputs[g][name][:].rearrange("r c i f -> r (c i f)").bitcast(F32)
-                    nc.tensor.transpose(
-                        words[:, ip, u, :], all_words[:, first_word : first_word + P], ident_f32[:]
-                    )
-            nc.scalar.copy(
-                out=xc_grouped[:, 0:part].bitcast(F32).rearrange("q (ip r u) -> q ip r u", ip=PAIRS, u=2),
-                in_=words[:].rearrange("q ip u r -> q ip r u"),
-            )
-
-            planes = psum_t.tile([P, PAIRS, PACK, P], BF16)
-            for ip in range(PAIRS):
-                for u, rows in enumerate((inputs[g]["xt2"], xt3_rows[g])):
-                    pair = rows[:, k, 2 * ip : 2 * ip + 2, :].rearrange("r i (w e) -> r (i w) e", e=2)
-                    for e in range(2):
-                        nc.tensor.transpose(planes[:, ip, 2 * u + e, :], pair[:, :, e], ident_bf16[:])
-            nc.scalar.copy(
-                out=xc_grouped[:, part : 2 * part].rearrange("q (ip r t) -> q ip r t", ip=PAIRS, t=PACK),
-                in_=planes[:].rearrange("q ip t r -> q ip r t"),
-            )
+            for s, pair in enumerate(
+                ((inputs[g]["x"], inputs[g]["x1"]), (inputs[g]["xt2"], xt3_rows[g]))
+            ):
+                words = psum_t.tile([P, PAIRS, 2, P], F32, name="turned")
+                for ip in range(PAIRS):
+                    first_word = (k * ROWS + 2 * ip) * (FEAT // 2)
+                    for u, rows in enumerate(pair):
+                        all_words = rows[:].rearrange("r c i f -> r (c i f)").bitcast(F32)
+                        nc.tensor.transpose(
+                            words[:, ip, u, :], all_words[:, first_word : first_word + P], ident_f32[:]
+                        )
+                nc.scalar.copy(
+                    out=xc_grouped[:, s * part : (s + 1) * part]
+                    .bitcast(F32)
+                    .rearrange("q (ip r u) -> q ip r u", ip=PAIRS, u=2),
+                    in_=words[:].rearrange("q ip u r -> q ip r u"),
+                )
             return xc_grouped
 
         def quantise_item(c, xc_grouped):

@@ -23,6 +23,7 @@ GROUP = 4
 N_GROUPS = BATCH // GROUP
 LOAD_BUFS = 6
 LOAD_AHEAD = LOAD_BUFS - 1
+OUT_BUFS = 12
 LAG = 2
 
 FLOPS = 2 * BATCH * NODES * NODES * FEAT + 2 * BATCH * NODES * ORDERS * FEAT * FEAT
@@ -35,6 +36,7 @@ def tile_gcncheb_pb_t_kernel(tc, x, x1, x2, xt2, L, weight, bias, out):
         loads = ctx.enter_context(tc.tile_pool(name="loads", bufs=LOAD_BUFS))
         per_group = ctx.enter_context(tc.tile_pool(name="per_group", bufs=2))
         per_item = ctx.enter_context(tc.tile_pool(name="per_item", bufs=LAG + 2))
+        results = ctx.enter_context(tc.tile_pool(name="results", bufs=OUT_BUFS))
         psum_x3 = ctx.enter_context(tc.psum_pool(name="psum_x3", bufs=2))
         psum_t = ctx.enter_context(tc.psum_pool(name="psum_t", bufs=4))
         psum_out = ctx.enter_context(tc.psum_pool(name="psum_out", bufs=2))
@@ -203,9 +205,9 @@ def tile_gcncheb_pb_t_kernel(tc, x, x1, x2, xt2, L, weight, bias, out):
                         start=(s == 0),
                         stop=(s == 1),
                     )
-            out_rows = per_item.tile([P, ROWS * FEAT], F32)
+            out_rows = results.tile([P, ROWS * FEAT], F32)
             nc.vector.tensor_tensor(out=out_rows[:], in0=acc[:], in1=bias_rows[:], op=ALU.add)
-            nc.gpsimd.dma_start(out=out[c].rearrange("(r i) o -> r (i o)", i=ROWS), in_=out_rows[:])
+            nc.sync.dma_start(out=out[c].rearrange("(r i) o -> r (i o)", i=ROWS), in_=out_rows[:])
 
         quantise_x2(0)
         for i in range(ROWS):

@@ -34,7 +34,7 @@ def tile_gcncheb_pb_t_kernel(tc, x, x1, x2, xt2, L, weight, bias, out):
     with ExitStack() as ctx:
         const = ctx.enter_context(tc.tile_pool(name="const", bufs=1))
         loads = ctx.enter_context(tc.tile_pool(name="loads", bufs=LOAD_BUFS))
-        per_group = ctx.enter_context(tc.tile_pool(name="per_group", bufs=2))
+        per_group = ctx.enter_context(tc.tile_pool(name="per_group", bufs=3))
         per_item = ctx.enter_context(tc.tile_pool(name="per_item", bufs=LAG + 2))
         results = ctx.enter_context(tc.tile_pool(name="results", bufs=OUT_BUFS))
         psum_x3 = ctx.enter_context(tc.psum_pool(name="psum_x3", bufs=2))
@@ -60,7 +60,11 @@ def tile_gcncheb_pb_t_kernel(tc, x, x1, x2, xt2, L, weight, bias, out):
             }
 
         l_rows = const.tile([P, ROWS, NODES], BF16)
-        nc.sync.dma_start(out=l_rows[:], in_=L.rearrange("(r i) m -> r i m", i=ROWS))
+        for ip in range(PAIRS):
+            pair = slice(2 * ip, 2 * ip + 2)
+            nc.sync.dma_start(
+                out=l_rows[:, pair], in_=L.rearrange("(r i) m -> r i m", i=ROWS)[:, pair]
+            )
         load_inputs(0)
         w_rows = const.tile([P, ORDERS, 2, FEAT], BF16)
         for h in range(2):
@@ -79,60 +83,47 @@ def tile_gcncheb_pb_t_kernel(tc, x, x1, x2, xt2, L, weight, bias, out):
         make_identity(nc, ident_f32[:])
 
         l_grouped = const.tile([P, ROWS, P, PACK], BF16, align_bytes=64)
+        l_codes = const.tile([P, ROWS * P], U32, align_bytes=64)
+        l_scales = const.tile([P, ROWS * P], U8, align_bytes=64)
         for ip in range(PAIRS):
             l_planes = psum_t.tile([P, 2, PACK, P], BF16, name="turned")
             for i2 in range(2):
                 l_cols = l_rows[:, 2 * ip + i2, :].rearrange("r (p t) -> r p t", t=PACK)
                 for t in range(PACK):
                     nc.tensor.transpose(l_planes[:, i2, t, :], l_cols[:, :, t], ident_bf16[:])
-            nc.scalar.copy(
+            copy = nc.scalar.copy if ip == 0 else nc.vector.tensor_copy
+            copy(
                 out=l_grouped[:, 2 * ip : 2 * ip + 2],
                 in_=l_planes[:].rearrange("p i t r -> p i r t"),
             )
-        l_codes = const.tile([P, ROWS * P], U32, align_bytes=64)
-        l_scales = const.tile([P, ROWS * P], U8, align_bytes=64)
-        nc.vector.quantize_mx(
-            out=l_codes[:].bitcast(FP8X4),
-            scales=l_scales[:],
-            in_=l_grouped[:].rearrange("p i r t -> p (i r t)"),
-        )
+            cols = slice(2 * ip * P, 2 * (ip + 1) * P)
+            nc.vector.quantize_mx(
+                out=l_codes[:, cols].bitcast(FP8X4),
+                scales=l_scales[:, cols],
+                in_=l_grouped[:, 2 * ip : 2 * ip + 2].rearrange("p i r t -> p (i r t)"),
+            )
 
-        w_grouped = const.tile([P, 2, 2, FEAT, PACK], BF16, align_bytes=64)
-        nc.vector.memset(w_grouped[:], 0.0)
-        for h in range(2):
-            half = slice(h * HALF, (h + 1) * HALF)
-            for s in range(2):
-                nc.vector.tensor_copy(
-                    out=w_grouped[half, s, h].rearrange("q o (u e) -> q o u e", u=2),
-                    in_=w_rows[half, 2 * s : 2 * s + 2].rearrange("q u e o -> q o u e"),
-                )
-        w_codes = const.tile([P, 2 * 2 * FEAT], U32, align_bytes=64)
-        w_scales = const.tile([P, 2 * 2 * FEAT], U8, align_bytes=64)
-        nc.vector.quantize_mx(
-            out=w_codes[:].bitcast(FP8X4),
-            scales=w_scales[:],
-            in_=w_grouped[:].rearrange("q s i o t -> q (s i o t)"),
-        )
-
+        x2_grouped = {}
         x2_quantised = {}
         xt3_rows = {}
         xc_quantised = {}
+        def regroup_x2(g, copy, items):
+            if g not in x2_grouped:
+                x2_grouped[g] = per_group.tile(
+                    [P, GROUP, FEAT, PACK], BF16, align_bytes=64, name="x2_grouped"
+                )
+            copy(
+                out=x2_grouped[g][:, items],
+                in_=inputs[g]["x2"][:, items].rearrange("p c j f -> p c f j"),
+            )
 
         def quantise_x2(g):
-            x2_rows = inputs[g]["x2"]
-            x2_grouped = per_group.tile([P, GROUP, FEAT, PACK], BF16, align_bytes=64)
-            nc.vector.tensor_copy(
-                out=x2_grouped[:, 0:2], in_=x2_rows[:, 0:2].rearrange("p c j f -> p c f j")
-            )
-            nc.scalar.copy(
-                out=x2_grouped[:, 2:4], in_=x2_rows[:, 2:4].rearrange("p c j f -> p c f j")
-            )
             x2_codes = per_group.tile([P, GROUP * FEAT], U32, align_bytes=64)
             x2_scales = per_group.tile([P, GROUP * FEAT], U8, align_bytes=64)
             nc.vector.quantize_mx(
                 out=x2_codes[:].bitcast(FP8X4),
                 scales=x2_scales[:],
-                in_=x2_grouped[:].rearrange("p c f j -> p (c f j)"),
+                in_=x2_grouped[g][:].rearrange("p c f j -> p (c f j)"),
             )
             x2_quantised[g] = (x2_codes, x2_scales)
             xt3_rows[g] = per_group.tile([P, GROUP, ROWS, FEAT], BF16, name="xt3_rows")
@@ -209,19 +200,43 @@ def tile_gcncheb_pb_t_kernel(tc, x, x1, x2, xt2, L, weight, bias, out):
             nc.vector.tensor_tensor(out=out_rows[:], in0=acc[:], in1=bias_rows[:], op=ALU.add)
             nc.sync.dma_start(out=out[c].rearrange("(r i) o -> r (i o)", i=ROWS), in_=out_rows[:])
 
+        regroup_x2(0, nc.vector.tensor_copy, slice(0, 2))
+        regroup_x2(0, nc.scalar.copy, slice(2, 4))
         quantise_x2(0)
         for i in range(ROWS):
             recurrence(0, i)
+        regroup_x2(1, nc.scalar.copy, slice(0, GROUP))
+        quantise_x2(1)
+
+        w_grouped = const.tile([P, 2, 2, FEAT, PACK], BF16, align_bytes=64)
+        nc.vector.memset(w_grouped[:], 0.0)
+        for h in range(2):
+            half = slice(h * HALF, (h + 1) * HALF)
+            for s in range(2):
+                nc.vector.tensor_copy(
+                    out=w_grouped[half, s, h].rearrange("q o (u e) -> q o u e", u=2),
+                    in_=w_rows[half, 2 * s : 2 * s + 2].rearrange("q u e o -> q o u e"),
+                )
+        w_codes = const.tile([P, 2 * 2 * FEAT], U32, align_bytes=64)
+        w_scales = const.tile([P, 2 * 2 * FEAT], U8, align_bytes=64)
+        nc.vector.quantize_mx(
+            out=w_codes[:].bitcast(FP8X4),
+            scales=w_scales[:],
+            in_=w_grouped[:].rearrange("q s i o t -> q (s i o t)"),
+        )
+
         for c in range(BATCH + LAG):
             g, k = divmod(c, GROUP)
             if c < BATCH:
                 if k == 0 and g + LOAD_AHEAD < N_GROUPS:
                     load_inputs(g + LOAD_AHEAD)
-                if k == 0 and g + 1 < N_GROUPS:
-                    quantise_x2(g + 1)
                 xc_grouped = transpose_item(c)
                 if g + 1 < N_GROUPS:
                     recurrence(g + 1, k)
                 quantise_item(c, xc_grouped)
+                if g + 2 < N_GROUPS:
+                    regroup_x2(g + 2, nc.scalar.copy, slice(k, k + 1))
+                    if k == GROUP - 1:
+                        quantise_x2(g + 2)
             if c >= LAG:
                 filter_item(c - LAG)

@@ -40,6 +40,7 @@ def tile_gcncheb_pb_t_kernel(tc, x, x1, x2, xt2, L, weight, bias, out):
         psum_x3 = ctx.enter_context(tc.psum_pool(name="psum_x3", bufs=2))
         psum_t = ctx.enter_context(tc.psum_pool(name="psum_t", bufs=4))
         psum_out = ctx.enter_context(tc.psum_pool(name="psum_out", bufs=2))
+        ctx.enter_context(tc.manual_schedule())
 
         def load_group(src, g, name):
             rows = loads.tile([P, GROUP, ROWS, FEAT], BF16, name=name)
@@ -49,12 +50,15 @@ def tile_gcncheb_pb_t_kernel(tc, x, x1, x2, xt2, L, weight, bias, out):
             )
             return rows
 
+        x2_rows = {}
         inputs = {}
 
         def load_inputs(g):
+            x1_rows = load_group(x1, g, "x1_rows")
+            if g + 1 < N_GROUPS:
+                x2_rows[g + 1] = load_group(x2, g + 1, "x2_rows")
             inputs[g] = {
-                "x2": load_group(x2, g, "x2_rows"),
-                "x1": load_group(x1, g, "x1_rows"),
+                "x1": x1_rows,
                 "x": load_group(x, g, "x_rows"),
                 "xt2": load_group(xt2, g, "xt2_rows"),
             }
@@ -65,6 +69,7 @@ def tile_gcncheb_pb_t_kernel(tc, x, x1, x2, xt2, L, weight, bias, out):
             nc.sync.dma_start(
                 out=l_rows[:, pair], in_=L.rearrange("(r i) m -> r i m", i=ROWS)[:, pair]
             )
+        x2_rows[0] = load_group(x2, 0, "x2_rows")
         load_inputs(0)
         w_rows = const.tile([P, ORDERS, 2, FEAT], BF16)
         for h in range(2):
@@ -82,20 +87,45 @@ def tile_gcncheb_pb_t_kernel(tc, x, x1, x2, xt2, L, weight, bias, out):
         ident_f32 = const.tile([P, P], F32)
         make_identity(nc, ident_f32[:])
 
+        w_grouped = const.tile([P, 2, 2, FEAT, PACK], BF16, align_bytes=64)
+        nc.gpsimd.memset(w_grouped[:].rearrange("q s i o t -> q (s i o t)").bitcast(U32), 0)
+        for h in range(2):
+            half = slice(h * HALF, (h + 1) * HALF)
+            for s in range(2):
+                nc.gpsimd.tensor_scalar(
+                    out=w_grouped[half, s, h].rearrange("q o (u e) -> q o u e", u=2),
+                    in0=w_rows[half, 2 * s : 2 * s + 2].rearrange("q u e o -> q o u e"),
+                    scalar1=1.0,
+                    scalar2=0.0,
+                    op0=ALU.mult,
+                    op1=ALU.add,
+                )
+        w_codes = const.tile([P, 2 * 2 * FEAT], U32, align_bytes=64)
+        w_scales = const.tile([P, 2 * 2 * FEAT], U8, align_bytes=64)
+
+        def quantise_w():
+            nc.vector.quantize_mx(
+                out=w_codes[:].bitcast(FP8X4),
+                scales=w_scales[:],
+                in_=w_grouped[:].rearrange("q s i o t -> q (s i o t)"),
+            )
+
         l_grouped = const.tile([P, ROWS, P, PACK], BF16, align_bytes=64)
         l_codes = const.tile([P, ROWS * P], U32, align_bytes=64)
         l_scales = const.tile([P, ROWS * P], U8, align_bytes=64)
-        for ip in range(PAIRS):
+
+        def turn_l(ip, copy):
             l_planes = psum_t.tile([P, 2, PACK, P], BF16, name="turned")
             for i2 in range(2):
                 l_cols = l_rows[:, 2 * ip + i2, :].rearrange("r (p t) -> r p t", t=PACK)
                 for t in range(PACK):
                     nc.tensor.transpose(l_planes[:, i2, t, :], l_cols[:, :, t], ident_bf16[:])
-            copy = nc.scalar.copy if ip == 0 else nc.vector.tensor_copy
             copy(
                 out=l_grouped[:, 2 * ip : 2 * ip + 2],
                 in_=l_planes[:].rearrange("p i t r -> p i r t"),
             )
+
+        def quantise_l(ip):
             cols = slice(2 * ip * P, 2 * (ip + 1) * P)
             nc.vector.quantize_mx(
                 out=l_codes[:, cols].bitcast(FP8X4),
@@ -106,7 +136,9 @@ def tile_gcncheb_pb_t_kernel(tc, x, x1, x2, xt2, L, weight, bias, out):
         x2_grouped = {}
         x2_quantised = {}
         xt3_rows = {}
+        xc_grouped = {}
         xc_quantised = {}
+
         def regroup_x2(g, copy, items):
             if g not in x2_grouped:
                 x2_grouped[g] = per_group.tile(
@@ -114,7 +146,7 @@ def tile_gcncheb_pb_t_kernel(tc, x, x1, x2, xt2, L, weight, bias, out):
                 )
             copy(
                 out=x2_grouped[g][:, items],
-                in_=inputs[g]["x2"][:, items].rearrange("p c j f -> p c f j"),
+                in_=x2_rows[g][:, items].rearrange("p c j f -> p c f j"),
             )
 
         def quantise_x2(g):
@@ -126,9 +158,10 @@ def tile_gcncheb_pb_t_kernel(tc, x, x1, x2, xt2, L, weight, bias, out):
                 in_=x2_grouped[g][:].rearrange("p c f j -> p (c f j)"),
             )
             x2_quantised[g] = (x2_codes, x2_scales)
-            xt3_rows[g] = per_group.tile([P, GROUP, ROWS, FEAT], BF16, name="xt3_rows")
 
         def recurrence(g, i):
+            if i == 0:
+                xt3_rows[g] = per_group.tile([P, GROUP, ROWS, FEAT], BF16, name="xt3_rows")
             x2_codes, x2_scales = x2_quantised[g]
             node_cols = slice(i * P, (i + 1) * P)
             x3 = psum_x3.tile([P, GROUP * FEAT], F32)
@@ -150,34 +183,37 @@ def tile_gcncheb_pb_t_kernel(tc, x, x1, x2, xt2, L, weight, bias, out):
                 op1=ALU.subtract,
             )
 
-        def transpose_item(c):
+        def turn_item(c, s):
             g, k = divmod(c, GROUP)
-            xc_grouped = per_item.tile([P, 2 * PAIRS * P * PACK], BF16, align_bytes=64)
-            part = PAIRS * P * PACK
-
-            for s, pair in enumerate(
-                ((inputs[g]["x"], inputs[g]["x1"]), (inputs[g]["xt2"], xt3_rows[g]))
-            ):
-                words = psum_t.tile([P, PAIRS, 2, P], F32, name="turned")
-                for ip in range(PAIRS):
-                    first_word = (k * ROWS + 2 * ip) * (FEAT // 2)
-                    for u, rows in enumerate(pair):
-                        all_words = rows[:].rearrange("r c i f -> r (c i f)").bitcast(F32)
-                        nc.tensor.transpose(
-                            words[:, ip, u, :], all_words[:, first_word : first_word + P], ident_f32[:]
-                        )
-                nc.scalar.copy(
-                    out=xc_grouped[:, s * part : (s + 1) * part]
-                    .bitcast(F32)
-                    .rearrange("q (ip r u) -> q ip r u", ip=PAIRS, u=2),
-                    in_=words[:].rearrange("q ip u r -> q ip r u"),
+            if s == 0:
+                xc_grouped[c] = per_item.tile(
+                    [P, 2 * PAIRS * P * PACK], BF16, align_bytes=64, name="xc_grouped"
                 )
-            return xc_grouped
+                pair = (inputs[g]["x"], inputs[g]["x1"])
+            else:
+                pair = (inputs[g]["xt2"], xt3_rows[g])
+            part = PAIRS * P * PACK
+            words = psum_t.tile([P, PAIRS, 2, P], F32, name="turned")
+            for ip in range(PAIRS):
+                first_word = (k * ROWS + 2 * ip) * (FEAT // 2)
+                for u, rows in enumerate(pair):
+                    all_words = rows[:].rearrange("r c i f -> r (c i f)").bitcast(F32)
+                    nc.tensor.transpose(
+                        words[:, ip, u, :], all_words[:, first_word : first_word + P], ident_f32[:]
+                    )
+            nc.scalar.copy(
+                out=xc_grouped[c][:, s * part : (s + 1) * part]
+                .bitcast(F32)
+                .rearrange("q (ip r u) -> q ip r u", ip=PAIRS, u=2),
+                in_=words[:].rearrange("q ip u r -> q ip r u"),
+            )
 
-        def quantise_item(c, xc_grouped):
+        def quantise_item(c):
             xc_codes = per_item.tile([P, 2 * PAIRS * P], U32, align_bytes=64)
             xc_scales = per_item.tile([P, 2 * PAIRS * P], U8, align_bytes=64)
-            nc.vector.quantize_mx(out=xc_codes[:].bitcast(FP8X4), scales=xc_scales[:], in_=xc_grouped[:])
+            nc.vector.quantize_mx(
+                out=xc_codes[:].bitcast(FP8X4), scales=xc_scales[:], in_=xc_grouped[c][:]
+            )
             xc_quantised[c] = (xc_codes, xc_scales)
 
         def filter_item(c):
@@ -196,47 +232,48 @@ def tile_gcncheb_pb_t_kernel(tc, x, x1, x2, xt2, L, weight, bias, out):
                         start=(s == 0),
                         stop=(s == 1),
                     )
+            return acc
+
+        def finish_item(c, acc):
             out_rows = results.tile([P, ROWS * FEAT], F32)
             nc.vector.tensor_tensor(out=out_rows[:], in0=acc[:], in1=bias_rows[:], op=ALU.add)
             nc.sync.dma_start(out=out[c].rearrange("(r i) o -> r (i o)", i=ROWS), in_=out_rows[:])
 
+        turn_l(0, nc.scalar.copy)
         regroup_x2(0, nc.vector.tensor_copy, slice(0, 2))
         regroup_x2(0, nc.scalar.copy, slice(2, 4))
+        quantise_l(0)
+        turn_l(1, nc.vector.tensor_copy)
         quantise_x2(0)
+        quantise_l(1)
+        turn_item(0, 0)
         for i in range(ROWS):
             recurrence(0, i)
-        regroup_x2(1, nc.scalar.copy, slice(0, GROUP))
+        regroup_x2(1, nc.vector.tensor_copy, slice(0, 2))
+        regroup_x2(1, nc.scalar.copy, slice(2, 4))
+        quantise_w()
         quantise_x2(1)
-
-        w_grouped = const.tile([P, 2, 2, FEAT, PACK], BF16, align_bytes=64)
-        nc.vector.memset(w_grouped[:], 0.0)
-        for h in range(2):
-            half = slice(h * HALF, (h + 1) * HALF)
-            for s in range(2):
-                nc.vector.tensor_copy(
-                    out=w_grouped[half, s, h].rearrange("q o (u e) -> q o u e", u=2),
-                    in_=w_rows[half, 2 * s : 2 * s + 2].rearrange("q u e o -> q o u e"),
-                )
-        w_codes = const.tile([P, 2 * 2 * FEAT], U32, align_bytes=64)
-        w_scales = const.tile([P, 2 * 2 * FEAT], U8, align_bytes=64)
-        nc.vector.quantize_mx(
-            out=w_codes[:].bitcast(FP8X4),
-            scales=w_scales[:],
-            in_=w_grouped[:].rearrange("q s i o t -> q (s i o t)"),
-        )
 
         for c in range(BATCH + LAG):
             g, k = divmod(c, GROUP)
-            if c < BATCH:
-                if k == 0 and g + LOAD_AHEAD < N_GROUPS:
-                    load_inputs(g + LOAD_AHEAD)
-                xc_grouped = transpose_item(c)
-                if g + 1 < N_GROUPS:
-                    recurrence(g + 1, k)
-                quantise_item(c, xc_grouped)
-                if g + 2 < N_GROUPS:
-                    regroup_x2(g + 2, nc.scalar.copy, slice(k, k + 1))
-                    if k == GROUP - 1:
-                        quantise_x2(g + 2)
+            if k == 0 and g + LOAD_AHEAD < N_GROUPS:
+                load_inputs(g + LOAD_AHEAD)
             if c >= LAG:
-                filter_item(c - LAG)
+                acc = filter_item(c - LAG)
+            if c < BATCH:
+                if c > 0:
+                    turn_item(c, 0)
+                turn_item(c, 1)
+            if 0 < c <= BATCH:
+                quantise_item(c - 1)
+            if c >= LAG:
+                finish_item(c - LAG, acc)
+            if g + 1 < N_GROUPS:
+                recurrence(g + 1, k)
+            g_next, k_next = divmod(c + 1, GROUP)
+            if c in (1, 2):
+                regroup_x2(2, nc.scalar.copy, slice(2 * c - 2, 2 * c))
+            elif g_next > 0 and g_next + 2 < N_GROUPS:
+                regroup_x2(g_next + 2, nc.scalar.copy, slice(k_next, k_next + 1))
+            if k == GROUP - 1 and g + 2 < N_GROUPS:
+                quantise_x2(g + 2)

@@ -21,8 +21,8 @@ ROWS = NODES // P
 PAIRS = ROWS // 2
 GROUP = 4
 N_GROUPS = BATCH // GROUP
-LOAD_BUFS = 6
-LOAD_AHEAD = LOAD_BUFS - 1
+LOAD_AHEAD = 3
+LOAD_BUFS = LOAD_AHEAD + 2
 OUT_BUFS = 12
 LAG = 2
 
@@ -53,15 +53,16 @@ def tile_gcncheb_pb_t_kernel(tc, x, x1, x2, xt2, L, weight, bias, out):
         x2_rows = {}
         inputs = {}
 
-        def load_inputs(g):
-            x1_rows = load_group(x1, g, "x1_rows")
-            if g + 1 < N_GROUPS:
-                x2_rows[g + 1] = load_group(x2, g + 1, "x2_rows")
-            inputs[g] = {
-                "x1": x1_rows,
-                "x": load_group(x, g, "x_rows"),
-                "xt2": load_group(xt2, g, "xt2_rows"),
-            }
+        def load_part(g, k):
+            if k == 0:
+                inputs[g] = {"x1": load_group(x1, g, "x1_rows")}
+            elif k == 1:
+                if g + 1 < N_GROUPS:
+                    x2_rows[g + 1] = load_group(x2, g + 1, "x2_rows")
+            elif k == 2:
+                inputs[g]["x"] = load_group(x, g, "x_rows")
+            else:
+                inputs[g]["xt2"] = load_group(xt2, g, "xt2_rows")
 
         l_rows = const.tile([P, ROWS, NODES], BF16)
         for ip in range(PAIRS):
@@ -70,7 +71,8 @@ def tile_gcncheb_pb_t_kernel(tc, x, x1, x2, xt2, L, weight, bias, out):
                 out=l_rows[:, pair], in_=L.rearrange("(r i) m -> r i m", i=ROWS)[:, pair]
             )
         x2_rows[0] = load_group(x2, 0, "x2_rows")
-        load_inputs(0)
+        for k in range(4):
+            load_part(0, k)
         w_rows = const.tile([P, ORDERS, 2, FEAT], BF16)
         for h in range(2):
             nc.sync.dma_start(
@@ -80,7 +82,8 @@ def tile_gcncheb_pb_t_kernel(tc, x, x1, x2, xt2, L, weight, bias, out):
         bias_rows = const.tile([P, ROWS * FEAT], BF16)
         nc.sync.dma_start(out=bias_rows[:], in_=bias[0].rearrange("(r i) o -> r (i o)", i=ROWS))
         for g in range(1, LOAD_AHEAD):
-            load_inputs(g)
+            for k in range(4):
+                load_part(g, k)
 
         ident_bf16 = const.tile([P, P], BF16)
         make_identity(nc, ident_bf16[:])
@@ -235,9 +238,12 @@ def tile_gcncheb_pb_t_kernel(tc, x, x1, x2, xt2, L, weight, bias, out):
             return acc
 
         def finish_item(c, acc):
-            out_rows = results.tile([P, ROWS * FEAT], F32)
-            nc.vector.tensor_tensor(out=out_rows[:], in0=acc[:], in1=bias_rows[:], op=ALU.add)
-            nc.sync.dma_start(out=out[c].rearrange("(r i) o -> r (i o)", i=ROWS), in_=out_rows[:])
+            rows = results.tile([P, ROWS * FEAT], F32)
+            nc.vector.tensor_tensor(out=rows[:], in0=acc[:], in1=bias_rows[:], op=ALU.add)
+            return rows
+
+        def store_item(c, rows):
+            nc.scalar.dma_start(out=out[c].rearrange("(r i) o -> r (i o)", i=ROWS), in_=rows[:])
 
         turn_l(0, nc.scalar.copy)
         regroup_x2(0, nc.vector.tensor_copy, slice(0, 2))
@@ -254,10 +260,13 @@ def tile_gcncheb_pb_t_kernel(tc, x, x1, x2, xt2, L, weight, bias, out):
         quantise_w()
         quantise_x2(1)
 
+        out_rows = {}
         for c in range(BATCH + LAG):
             g, k = divmod(c, GROUP)
-            if k == 0 and g + LOAD_AHEAD < N_GROUPS:
-                load_inputs(g + LOAD_AHEAD)
+            if g + LOAD_AHEAD < N_GROUPS:
+                load_part(g + LOAD_AHEAD, k)
+            if c > LAG:
+                store_item(c - LAG - 1, out_rows[c - LAG - 1])
             if c >= LAG:
                 acc = filter_item(c - LAG)
             if c < BATCH:
@@ -267,7 +276,7 @@ def tile_gcncheb_pb_t_kernel(tc, x, x1, x2, xt2, L, weight, bias, out):
             if 0 < c <= BATCH:
                 quantise_item(c - 1)
             if c >= LAG:
-                finish_item(c - LAG, acc)
+                out_rows[c - LAG] = finish_item(c - LAG, acc)
             if g + 1 < N_GROUPS:
                 recurrence(g + 1, k)
             g_next, k_next = divmod(c + 1, GROUP)
@@ -277,3 +286,4 @@ def tile_gcncheb_pb_t_kernel(tc, x, x1, x2, xt2, L, weight, bias, out):
                 regroup_x2(g_next + 2, nc.scalar.copy, slice(k_next, k_next + 1))
             if k == GROUP - 1 and g + 2 < N_GROUPS:
                 quantise_x2(g + 2)
+        store_item(BATCH - 1, out_rows[BATCH - 1])

@@ -23,8 +23,7 @@ GROUP = 4
 N_GROUPS = BATCH // GROUP
 LOAD_AHEAD = 3
 LOAD_BUFS = LOAD_AHEAD + 2
-OUT_BUFS = 12
-LAG = 2
+LAG = 3
 
 FLOPS = 2 * BATCH * NODES * NODES * FEAT + 2 * BATCH * NODES * ORDERS * FEAT * FEAT
 
@@ -36,7 +35,7 @@ def tile_gcncheb_pb_t_kernel(tc, x, x1, x2, xt2, L, weight, bias, out):
         loads = ctx.enter_context(tc.tile_pool(name="loads", bufs=LOAD_BUFS))
         per_group = ctx.enter_context(tc.tile_pool(name="per_group", bufs=3))
         per_item = ctx.enter_context(tc.tile_pool(name="per_item", bufs=LAG + 2))
-        results = ctx.enter_context(tc.tile_pool(name="results", bufs=OUT_BUFS))
+        results = ctx.enter_context(tc.tile_pool(name="results", bufs=BATCH))
         psum_x3 = ctx.enter_context(tc.psum_pool(name="psum_x3", bufs=2))
         psum_t = ctx.enter_context(tc.psum_pool(name="psum_t", bufs=4))
         psum_out = ctx.enter_context(tc.psum_pool(name="psum_out", bufs=2))
@@ -243,7 +242,7 @@ def tile_gcncheb_pb_t_kernel(tc, x, x1, x2, xt2, L, weight, bias, out):
             return rows
 
         def store_item(c, rows):
-            nc.scalar.dma_start(out=out[c].rearrange("(r i) o -> r (i o)", i=ROWS), in_=rows[:])
+            nc.sync.dma_start(out=out[c].rearrange("(r i) o -> r (i o)", i=ROWS), in_=rows[:])
 
         turn_l(0, nc.scalar.copy)
         regroup_x2(0, nc.vector.tensor_copy, slice(0, 2))
@@ -267,18 +266,16 @@ def tile_gcncheb_pb_t_kernel(tc, x, x1, x2, xt2, L, weight, bias, out):
                 load_part(g + LOAD_AHEAD, k)
             if c > LAG:
                 store_item(c - LAG - 1, out_rows[c - LAG - 1])
-            if c >= LAG:
-                acc = filter_item(c - LAG)
             if c < BATCH:
                 if c > 0:
                     turn_item(c, 0)
                 turn_item(c, 1)
             if 0 < c <= BATCH:
                 quantise_item(c - 1)
-            if c >= LAG:
-                out_rows[c - LAG] = finish_item(c - LAG, acc)
             if g + 1 < N_GROUPS:
                 recurrence(g + 1, k)
+            if c >= LAG:
+                out_rows[c - LAG] = finish_item(c - LAG, filter_item(c - LAG))
             g_next, k_next = divmod(c + 1, GROUP)
             if c in (1, 2):
                 regroup_x2(2, nc.scalar.copy, slice(2 * c - 2, 2 * c))

@@ -19,11 +19,11 @@ FEAT = 128
 ORDERS = 4
 ROWS = NODES // P
 PAIRS = ROWS // 2
-GROUP = 4
-N_GROUPS = BATCH // GROUP
-LOAD_AHEAD = 3
-LOAD_BUFS = LOAD_AHEAD + 2
-LAG = 3
+LOAD = 4
+LOAD_AHEAD = 4
+LOAD_BUFS = LOAD_AHEAD + 1
+REC_AHEAD = 2
+LAG = 2
 
 FLOPS = 2 * BATCH * NODES * NODES * FEAT + 2 * BATCH * NODES * ORDERS * FEAT * FEAT
 
@@ -33,35 +33,26 @@ def tile_gcncheb_pb_t_kernel(tc, x, x1, x2, xt2, L, weight, bias, out):
     with ExitStack() as ctx:
         const = ctx.enter_context(tc.tile_pool(name="const", bufs=1))
         loads = ctx.enter_context(tc.tile_pool(name="loads", bufs=LOAD_BUFS))
-        per_group = ctx.enter_context(tc.tile_pool(name="per_group", bufs=3))
-        per_item = ctx.enter_context(tc.tile_pool(name="per_item", bufs=LAG + 2))
+        x2_pairs = ctx.enter_context(tc.tile_pool(name="x2_pairs", bufs=3))
+        per_item = ctx.enter_context(tc.tile_pool(name="per_item", bufs=4))
         results = ctx.enter_context(tc.tile_pool(name="results", bufs=BATCH))
         psum_x3 = ctx.enter_context(tc.psum_pool(name="psum_x3", bufs=2))
         psum_t = ctx.enter_context(tc.psum_pool(name="psum_t", bufs=4))
         psum_out = ctx.enter_context(tc.psum_pool(name="psum_out", bufs=2))
         ctx.enter_context(tc.manual_schedule())
 
-        def load_group(src, g, name):
-            rows = loads.tile([P, GROUP, ROWS, FEAT], BF16, name=name)
+        sources = {"x": x, "x1": x1, "x2": x2, "xt2": xt2}
+        rows_of = {}
+
+        def load_items(name, first, count):
+            pool, tag = (loads, name) if first >= LOAD else (const, f"{name}_{first}")
+            rows = pool.tile([P, count, ROWS, FEAT], BF16, name=tag)
             nc.sync.dma_start(
                 out=rows[:],
-                in_=src[g * GROUP : (g + 1) * GROUP].rearrange("c (r i) f -> r c i f", i=ROWS),
+                in_=sources[name][first : first + count].rearrange("c (r i) f -> r c i f", i=ROWS),
             )
-            return rows
-
-        x2_rows = {}
-        inputs = {}
-
-        def load_part(g, k):
-            if k == 0:
-                inputs[g] = {"x1": load_group(x1, g, "x1_rows")}
-            elif k == 1:
-                if g + 1 < N_GROUPS:
-                    x2_rows[g + 1] = load_group(x2, g + 1, "x2_rows")
-            elif k == 2:
-                inputs[g]["x"] = load_group(x, g, "x_rows")
-            else:
-                inputs[g]["xt2"] = load_group(xt2, g, "xt2_rows")
+            for j in range(count):
+                rows_of[name, first + j] = rows[:, j]
 
         l_rows = const.tile([P, ROWS, NODES], BF16)
         for ip in range(PAIRS):
@@ -69,9 +60,15 @@ def tile_gcncheb_pb_t_kernel(tc, x, x1, x2, xt2, L, weight, bias, out):
             nc.sync.dma_start(
                 out=l_rows[:, pair], in_=L.rearrange("(r i) m -> r i m", i=ROWS)[:, pair]
             )
-        x2_rows[0] = load_group(x2, 0, "x2_rows")
-        for k in range(4):
-            load_part(0, k)
+        load_items("x2", 0, 2)
+        load_items("x1", 0, 2)
+        load_items("x", 0, 1)
+        load_items("xt2", 0, 1)
+        load_items("x2", 2, 2)
+        load_items("x", 1, 1)
+        load_items("xt2", 1, 1)
+        load_items("x1", 2, 2)
+        load_items("x2", LOAD, LOAD)
         w_rows = const.tile([P, ORDERS, 2, FEAT], BF16)
         for h in range(2):
             nc.sync.dma_start(
@@ -80,9 +77,14 @@ def tile_gcncheb_pb_t_kernel(tc, x, x1, x2, xt2, L, weight, bias, out):
             )
         bias_rows = const.tile([P, ROWS * FEAT], BF16)
         nc.sync.dma_start(out=bias_rows[:], in_=bias[0].rearrange("(r i) o -> r (i o)", i=ROWS))
-        for g in range(1, LOAD_AHEAD):
-            for k in range(4):
-                load_part(g, k)
+        load_items("x", 2, 2)
+        load_items("xt2", 2, 2)
+        for name in ("x1", "x", "xt2"):
+            load_items(name, LOAD, LOAD)
+        order_of_need = ("x2", "x1", "x", "xt2")
+        for first in range(2 * LOAD, LOAD_AHEAD * LOAD, LOAD):
+            for name in order_of_need:
+                load_items(name, first, LOAD)
 
         ident_bf16 = const.tile([P, P], BF16)
         make_identity(nc, ident_bf16[:])
@@ -91,19 +93,17 @@ def tile_gcncheb_pb_t_kernel(tc, x, x1, x2, xt2, L, weight, bias, out):
 
         w_grouped = const.tile([P, 2, 2, FEAT, PACK], BF16, align_bytes=64)
         nc.gpsimd.memset(w_grouped[:].rearrange("q s i o t -> q (s i o t)").bitcast(U32), 0)
-        for h in range(2):
-            half = slice(h * HALF, (h + 1) * HALF)
-            for s in range(2):
-                nc.gpsimd.tensor_scalar(
-                    out=w_grouped[half, s, h].rearrange("q o (u e) -> q o u e", u=2),
-                    in0=w_rows[half, 2 * s : 2 * s + 2].rearrange("q u e o -> q o u e"),
-                    scalar1=1.0,
-                    scalar2=0.0,
-                    op0=ALU.mult,
-                    op1=ALU.add,
-                )
         w_codes = const.tile([P, 2 * 2 * FEAT], U32, align_bytes=64)
         w_scales = const.tile([P, 2 * 2 * FEAT], U8, align_bytes=64)
+
+        def group_w():
+            for h in range(2):
+                half = slice(h * HALF, (h + 1) * HALF)
+                for s in range(2):
+                    nc.vector.tensor_copy(
+                        out=w_grouped[half, s, h].rearrange("q o (u e) -> q o u e", u=2),
+                        in_=w_rows[half, 2 * s : 2 * s + 2].rearrange("q u e o -> q o u e"),
+                    )
 
         def quantise_w():
             nc.vector.quantize_mx(
@@ -140,68 +140,68 @@ def tile_gcncheb_pb_t_kernel(tc, x, x1, x2, xt2, L, weight, bias, out):
         xt3_rows = {}
         xc_grouped = {}
         xc_quantised = {}
+        out_rows = {}
 
-        def regroup_x2(g, copy, items):
-            if g not in x2_grouped:
-                x2_grouped[g] = per_group.tile(
-                    [P, GROUP, FEAT, PACK], BF16, align_bytes=64, name="x2_grouped"
+        def regroup_x2(c, copy):
+            pair, j = divmod(c, 2)
+            if j == 0:
+                x2_grouped[pair] = x2_pairs.tile(
+                    [P, 2, FEAT, PACK], BF16, align_bytes=64, name="x2_grouped"
                 )
-            copy(
-                out=x2_grouped[g][:, items],
-                in_=x2_rows[g][:, items].rearrange("p c j f -> p c f j"),
-            )
+            copy(out=x2_grouped[pair][:, j], in_=rows_of["x2", c].rearrange("p i f -> p f i"))
 
-        def quantise_x2(g):
-            x2_codes = per_group.tile([P, GROUP * FEAT], U32, align_bytes=64)
-            x2_scales = per_group.tile([P, GROUP * FEAT], U8, align_bytes=64)
+        def quantise_x2(pair):
+            x2_codes = x2_pairs.tile([P, 2 * FEAT], U32, align_bytes=64)
+            x2_scales = x2_pairs.tile([P, 2 * FEAT], U8, align_bytes=64)
             nc.vector.quantize_mx(
                 out=x2_codes[:].bitcast(FP8X4),
                 scales=x2_scales[:],
-                in_=x2_grouped[g][:].rearrange("p c f j -> p (c f j)"),
+                in_=x2_grouped[pair][:].rearrange("p c f t -> p (c f t)"),
             )
-            x2_quantised[g] = (x2_codes, x2_scales)
+            x2_quantised[pair] = (x2_codes, x2_scales)
 
-        def recurrence(g, i):
-            if i == 0:
-                xt3_rows[g] = per_group.tile([P, GROUP, ROWS, FEAT], BF16, name="xt3_rows")
-            x2_codes, x2_scales = x2_quantised[g]
-            node_cols = slice(i * P, (i + 1) * P)
-            x3 = psum_x3.tile([P, GROUP * FEAT], F32)
-            nc.tensor.matmul_mx(
-                out=x3[:],
-                lhsT=l_codes[:, node_cols].bitcast(FP8X4),
-                lhsT_scale=l_scales[:, node_cols],
-                rhs=x2_codes[:].bitcast(FP8X4),
-                rhs_scale=x2_scales[:],
-                start=True,
-                stop=True,
-            )
+        def recurrence(c):
+            pair, j = divmod(c, 2)
+            x2_codes, x2_scales = x2_quantised[pair]
+            item_cols = slice(j * FEAT, (j + 1) * FEAT)
+            x3 = psum_x3.tile([P, ROWS * FEAT], F32)
+            for i in range(ROWS):
+                node_cols = slice(i * P, (i + 1) * P)
+                nc.tensor.matmul_mx(
+                    out=x3[:, i * FEAT : (i + 1) * FEAT],
+                    lhsT=l_codes[:, node_cols].bitcast(FP8X4),
+                    lhsT_scale=l_scales[:, node_cols],
+                    rhs=x2_codes[:, item_cols].bitcast(FP8X4),
+                    rhs_scale=x2_scales[:, item_cols],
+                    start=True,
+                    stop=True,
+                )
+            xt3_rows[c] = per_item.tile([P, ROWS * FEAT], BF16, name="xt3_rows")
             nc.vector.scalar_tensor_tensor(
-                out=xt3_rows[g][:, :, i, :],
-                in0=x3[:].rearrange("r (c f) -> r c f", f=FEAT),
+                out=xt3_rows[c][:],
+                in0=x3[:],
                 scalar=2.0,
-                in1=inputs[g]["x1"][:, :, i, :],
+                in1=rows_of["x1", c].rearrange("r i f -> r (i f)"),
                 op0=ALU.mult,
                 op1=ALU.subtract,
             )
 
         def turn_item(c, s):
-            g, k = divmod(c, GROUP)
             if s == 0:
                 xc_grouped[c] = per_item.tile(
                     [P, 2 * PAIRS * P * PACK], BF16, align_bytes=64, name="xc_grouped"
                 )
-                pair = (inputs[g]["x"], inputs[g]["x1"])
+                pair = [rows_of[name, c].rearrange("r i f -> r (i f)") for name in ("x", "x1")]
             else:
-                pair = (inputs[g]["xt2"], xt3_rows[g])
+                pair = [rows_of["xt2", c].rearrange("r i f -> r (i f)"), xt3_rows[c][:]]
             part = PAIRS * P * PACK
             words = psum_t.tile([P, PAIRS, 2, P], F32, name="turned")
             for ip in range(PAIRS):
-                first_word = (k * ROWS + 2 * ip) * (FEAT // 2)
-                for u, rows in enumerate(pair):
-                    all_words = rows[:].rearrange("r c i f -> r (c i f)").bitcast(F32)
+                for u in range(2):
                     nc.tensor.transpose(
-                        words[:, ip, u, :], all_words[:, first_word : first_word + P], ident_f32[:]
+                        words[:, ip, u, :],
+                        pair[u].bitcast(F32)[:, ip * P : (ip + 1) * P],
+                        ident_f32[:],
                     )
             nc.scalar.copy(
                 out=xc_grouped[c][:, s * part : (s + 1) * part]
@@ -234,53 +234,50 @@ def tile_gcncheb_pb_t_kernel(tc, x, x1, x2, xt2, L, weight, bias, out):
                         start=(s == 0),
                         stop=(s == 1),
                     )
-            return acc
+            out_rows[c] = results.tile([P, ROWS * FEAT], F32, name="out_rows")
+            nc.vector.tensor_tensor(out=out_rows[c][:], in0=acc[:], in1=bias_rows[:], op=ALU.add)
 
-        def finish_item(c, acc):
-            rows = results.tile([P, ROWS * FEAT], F32)
-            nc.vector.tensor_tensor(out=rows[:], in0=acc[:], in1=bias_rows[:], op=ALU.add)
-            return rows
-
-        def store_item(c, rows):
-            nc.sync.dma_start(out=out[c].rearrange("(r i) o -> r (i o)", i=ROWS), in_=rows[:])
+        def store_item(c):
+            nc.sync.dma_start(out=out[c].rearrange("(r i) o -> r (i o)", i=ROWS), in_=out_rows[c][:])
 
         turn_l(0, nc.scalar.copy)
-        regroup_x2(0, nc.vector.tensor_copy, slice(0, 2))
-        regroup_x2(0, nc.scalar.copy, slice(2, 4))
+        turn_l(1, nc.scalar.copy)
+        regroup_x2(0, nc.vector.tensor_copy)
+        regroup_x2(1, nc.vector.tensor_copy)
         quantise_l(0)
-        turn_l(1, nc.vector.tensor_copy)
         quantise_x2(0)
         quantise_l(1)
+        recurrence(0)
         turn_item(0, 0)
-        for i in range(ROWS):
-            recurrence(0, i)
-        regroup_x2(1, nc.vector.tensor_copy, slice(0, 2))
-        regroup_x2(1, nc.scalar.copy, slice(2, 4))
-        quantise_w()
+        regroup_x2(2, nc.vector.tensor_copy)
+        regroup_x2(3, nc.vector.tensor_copy)
+        recurrence(1)
         quantise_x2(1)
 
-        out_rows = {}
         for c in range(BATCH + LAG):
-            g, k = divmod(c, GROUP)
-            if g + LOAD_AHEAD < N_GROUPS:
-                load_part(g + LOAD_AHEAD, k)
+            group, k = divmod(c, LOAD)
+            if (group + LOAD_AHEAD) * LOAD < BATCH:
+                load_items(order_of_need[k], (group + LOAD_AHEAD) * LOAD, LOAD)
             if c > LAG:
-                store_item(c - LAG - 1, out_rows[c - LAG - 1])
+                store_item(c - LAG - 1)
+            if c % 2 == 1 and c + 3 < BATCH:
+                quantise_x2((c + 3) // 2)
             if c < BATCH:
                 if c > 0:
                     turn_item(c, 0)
                 turn_item(c, 1)
             if 0 < c <= BATCH:
                 quantise_item(c - 1)
-            if g + 1 < N_GROUPS:
-                recurrence(g + 1, k)
+            if c + REC_AHEAD < BATCH:
+                recurrence(c + REC_AHEAD)
+            if c == 0:
+                group_w()
+            if c == 1:
+                quantise_w()
             if c >= LAG:
-                out_rows[c - LAG] = finish_item(c - LAG, filter_item(c - LAG))
-            g_next, k_next = divmod(c + 1, GROUP)
-            if c in (1, 2):
-                regroup_x2(2, nc.scalar.copy, slice(2 * c - 2, 2 * c))
-            elif g_next > 0 and g_next + 2 < N_GROUPS:
-                regroup_x2(g_next + 2, nc.scalar.copy, slice(k_next, k_next + 1))
-            if k == GROUP - 1 and g + 2 < N_GROUPS:
-                quantise_x2(g + 2)
-        store_item(BATCH - 1, out_rows[BATCH - 1])
+                filter_item(c - LAG)
+            if c == 0:
+                regroup_x2(4, nc.scalar.copy)
+            if c + 5 < BATCH:
+                regroup_x2(c + 5, nc.scalar.copy)
+        store_item(BATCH - 1)

@@ -24,6 +24,12 @@ LOAD_AHEAD = 4
 LOAD_BUFS = LOAD_AHEAD + 1
 REC_AHEAD = 2
 LAG = 2
+STORE_LAG = LAG + 2
+
+
+def on_gpsimd(c):
+    return c % 4 == 1 and c < BATCH - 3
+
 
 FLOPS = 2 * BATCH * NODES * NODES * FEAT + 2 * BATCH * NODES * ORDERS * FEAT * FEAT
 
@@ -140,6 +146,7 @@ def tile_gcncheb_pb_t_kernel(tc, x, x1, x2, xt2, L, weight, bias, out):
         xt3_rows = {}
         xc_grouped = {}
         xc_quantised = {}
+        sums = {}
         out_rows = {}
 
         def regroup_x2(c, copy):
@@ -148,7 +155,10 @@ def tile_gcncheb_pb_t_kernel(tc, x, x1, x2, xt2, L, weight, bias, out):
                 x2_grouped[pair] = x2_pairs.tile(
                     [P, 2, FEAT, PACK], BF16, align_bytes=64, name="x2_grouped"
                 )
-            copy(out=x2_grouped[pair][:, j], in_=rows_of["x2", c].rearrange("p i f -> p f i"))
+            copy(
+                out=x2_grouped[pair][:, j].rearrange("p (q f) i -> p q i f", f=4),
+                in_=rows_of["x2", c].rearrange("p i (q f) -> p q i f", f=4),
+            )
 
         def quantise_x2(pair):
             x2_codes = x2_pairs.tile([P, 2 * FEAT], U32, align_bytes=64)
@@ -220,13 +230,13 @@ def tile_gcncheb_pb_t_kernel(tc, x, x1, x2, xt2, L, weight, bias, out):
 
         def filter_item(c):
             xc_codes, xc_scales = xc_quantised[c]
-            acc = psum_out.tile([P, ROWS * FEAT], F32)
+            sums[c] = psum_out.tile([P, ROWS * FEAT], F32, name="sums")
             for ip in range(PAIRS):
                 for s in range(2):
                     node_cols = slice((s * PAIRS + ip) * P, (s * PAIRS + ip + 1) * P)
                     w_cols = slice(s * 2 * FEAT, (s + 1) * 2 * FEAT)
                     nc.tensor.matmul_mx(
-                        out=acc[:, ip * 2 * FEAT : (ip + 1) * 2 * FEAT],
+                        out=sums[c][:, ip * 2 * FEAT : (ip + 1) * 2 * FEAT],
                         lhsT=xc_codes[:, node_cols].bitcast(FP8X4),
                         lhsT_scale=xc_scales[:, node_cols],
                         rhs=w_codes[:, w_cols].bitcast(FP8X4),
@@ -234,8 +244,24 @@ def tile_gcncheb_pb_t_kernel(tc, x, x1, x2, xt2, L, weight, bias, out):
                         start=(s == 0),
                         stop=(s == 1),
                     )
+
+        def add_bias(c):
             out_rows[c] = results.tile([P, ROWS * FEAT], F32, name="out_rows")
-            nc.vector.tensor_tensor(out=out_rows[c][:], in0=acc[:], in1=bias_rows[:], op=ALU.add)
+            nc.vector.tensor_tensor(
+                out=out_rows[c][:], in0=sums[c][:], in1=bias_rows[:], op=ALU.add
+            )
+
+        def add_bias_on_gpsimd(c):
+            out_rows[c] = results.tile([P, ROWS * FEAT], F32, name="out_rows")
+            nc.scalar.copy(out=out_rows[c][:], in_=sums[c][:])
+            for h in range(2):
+                cols = slice(h * ROWS * FEAT // 2, (h + 1) * ROWS * FEAT // 2)
+                nc.gpsimd.tensor_tensor(
+                    out=out_rows[c][:, cols],
+                    in0=out_rows[c][:, cols],
+                    in1=bias_rows[:, cols],
+                    op=ALU.add,
+                )
 
         def store_item(c):
             nc.sync.dma_start(out=out[c].rearrange("(r i) o -> r (i o)", i=ROWS), in_=out_rows[c][:])
@@ -258,8 +284,8 @@ def tile_gcncheb_pb_t_kernel(tc, x, x1, x2, xt2, L, weight, bias, out):
             group, k = divmod(c, LOAD)
             if (group + LOAD_AHEAD) * LOAD < BATCH:
                 load_items(order_of_need[k], (group + LOAD_AHEAD) * LOAD, LOAD)
-            if c > LAG:
-                store_item(c - LAG - 1)
+            if c >= STORE_LAG:
+                store_item(c - STORE_LAG)
             if c % 2 == 1 and c + 3 < BATCH:
                 quantise_x2((c + 3) // 2)
             if c < BATCH:
@@ -274,10 +300,15 @@ def tile_gcncheb_pb_t_kernel(tc, x, x1, x2, xt2, L, weight, bias, out):
                 group_w()
             if c == 1:
                 quantise_w()
+            if c > LAG and on_gpsimd(c - LAG - 1):
+                add_bias_on_gpsimd(c - LAG - 1)
             if c >= LAG:
                 filter_item(c - LAG)
+                if not on_gpsimd(c - LAG):
+                    add_bias(c - LAG)
             if c == 0:
                 regroup_x2(4, nc.scalar.copy)
             if c + 5 < BATCH:
                 regroup_x2(c + 5, nc.scalar.copy)
-        store_item(BATCH - 1)
+        for c in range(BATCH + LAG - STORE_LAG, BATCH):
+            store_item(c)

@@ -19,11 +19,13 @@ FEAT = 128
 ORDERS = 4
 ROWS = NODES // P
 PAIRS = ROWS // 2
+ITEM_COLS = 2 * PAIRS * P
 LOAD = 4
-LOAD_AHEAD = 4
+LOAD_AHEAD = 3
 LOAD_BUFS = LOAD_AHEAD + 1
 REC_AHEAD = 2
-LAG = 2
+LAG = 3
+OUT_BUFS = 28
 STORE_LAG = LAG + 2
 
 
@@ -40,18 +42,19 @@ def tile_gcncheb_pb_t_kernel(tc, x, x1, x2, xt2, L, weight, bias, out):
         const = ctx.enter_context(tc.tile_pool(name="const", bufs=1))
         loads = ctx.enter_context(tc.tile_pool(name="loads", bufs=LOAD_BUFS))
         x2_pairs = ctx.enter_context(tc.tile_pool(name="x2_pairs", bufs=3))
+        xc_pairs = ctx.enter_context(tc.tile_pool(name="xc_pairs", bufs=3))
         per_item = ctx.enter_context(tc.tile_pool(name="per_item", bufs=4))
-        results = ctx.enter_context(tc.tile_pool(name="results", bufs=BATCH))
+        results = ctx.enter_context(tc.tile_pool(name="results", bufs=OUT_BUFS))
         psum_x3 = ctx.enter_context(tc.psum_pool(name="psum_x3", bufs=2))
-        psum_t = ctx.enter_context(tc.psum_pool(name="psum_t", bufs=4))
-        psum_out = ctx.enter_context(tc.psum_pool(name="psum_out", bufs=2))
+        psum_t = ctx.enter_context(tc.psum_pool(name="psum_t", bufs=3))
+        psum_out = ctx.enter_context(tc.psum_pool(name="psum_out", bufs=3))
         ctx.enter_context(tc.manual_schedule())
 
         sources = {"x": x, "x1": x1, "x2": x2, "xt2": xt2}
         rows_of = {}
 
         def load_items(name, first, count):
-            pool, tag = (loads, name) if first >= LOAD else (const, f"{name}_{first}")
+            pool, tag = (loads, name) if count == LOAD and first > 0 else (const, f"{name}_{first}")
             rows = pool.tile([P, count, ROWS, FEAT], BF16, name=tag)
             nc.sync.dma_start(
                 out=rows[:],
@@ -66,31 +69,41 @@ def tile_gcncheb_pb_t_kernel(tc, x, x1, x2, xt2, L, weight, bias, out):
             nc.sync.dma_start(
                 out=l_rows[:, pair], in_=L.rearrange("(r i) m -> r i m", i=ROWS)[:, pair]
             )
-        load_items("x2", 0, 2)
+        load_items("x2", 0, 4)
         load_items("x1", 0, 2)
-        load_items("x", 0, 1)
-        load_items("xt2", 0, 1)
-        load_items("x2", 2, 2)
-        load_items("x", 1, 1)
-        load_items("xt2", 1, 1)
-        load_items("x1", 2, 2)
-        load_items("x2", LOAD, LOAD)
+        load_items("x", 0, 2)
+        load_items("xt2", 0, 2)
         w_rows = const.tile([P, ORDERS, 2, FEAT], BF16)
         for h in range(2):
             nc.sync.dma_start(
                 out=w_rows[h * HALF : (h + 1) * HALF],
                 in_=weight.rearrange("j (w e) o -> w j e o", e=2),
             )
-        bias_rows = const.tile([P, ROWS * FEAT], BF16)
-        nc.sync.dma_start(out=bias_rows[:], in_=bias[0].rearrange("(r i) o -> r (i o)", i=ROWS))
+        load_items("x1", 2, 2)
+        load_items("x2", 4, 2)
         load_items("x", 2, 2)
         load_items("xt2", 2, 2)
-        for name in ("x1", "x", "xt2"):
-            load_items(name, LOAD, LOAD)
-        order_of_need = ("x2", "x1", "x", "xt2")
-        for first in range(2 * LOAD, LOAD_AHEAD * LOAD, LOAD):
-            for name in order_of_need:
+        load_items("x2", 6, 2)
+        load_items("x1", 4, 2)
+        bias_rows = const.tile([P, ROWS * FEAT], BF16)
+        nc.sync.dma_start(out=bias_rows[:], in_=bias[0].rearrange("(r i) o -> r (i o)", i=ROWS))
+        load_items("x2", 8, 2)
+        load_items("x", 4, 2)
+        load_items("xt2", 4, 2)
+        load_items("x1", 6, 2)
+        load_items("x2", 10, 2)
+        load_items("x", 6, 2)
+        load_items("xt2", 6, 2)
+
+        def load_part(first, k):
+            name = ("x1", "x2", "x", "xt2")[k]
+            if name == "x2":
+                first += LOAD
+            if first < BATCH:
                 load_items(name, first, LOAD)
+
+        for k in range(4):
+            load_part(2 * LOAD, k)
 
         ident_bf16 = const.tile([P, P], BF16)
         make_identity(nc, ident_bf16[:])
@@ -198,13 +211,15 @@ def tile_gcncheb_pb_t_kernel(tc, x, x1, x2, xt2, L, weight, bias, out):
 
         def turn_item(c, s):
             if s == 0:
-                xc_grouped[c] = per_item.tile(
-                    [P, 2 * PAIRS * P * PACK], BF16, align_bytes=64, name="xc_grouped"
-                )
+                if c % 2 == 0:
+                    xc_grouped[c // 2] = xc_pairs.tile(
+                        [P, 2 * ITEM_COLS * PACK], BF16, align_bytes=64, name="xc_grouped"
+                    )
                 pair = [rows_of[name, c].rearrange("r i f -> r (i f)") for name in ("x", "x1")]
             else:
                 pair = [rows_of["xt2", c].rearrange("r i f -> r (i f)"), xt3_rows[c][:]]
-            part = PAIRS * P * PACK
+            part = ITEM_COLS * PACK // 2
+            start = (c % 2 * 2 + s) * part
             words = psum_t.tile([P, PAIRS, 2, P], F32, name="turned")
             for ip in range(PAIRS):
                 for u in range(2):
@@ -214,29 +229,37 @@ def tile_gcncheb_pb_t_kernel(tc, x, x1, x2, xt2, L, weight, bias, out):
                         ident_f32[:],
                     )
             nc.scalar.copy(
-                out=xc_grouped[c][:, s * part : (s + 1) * part]
+                out=xc_grouped[c // 2][:, start : start + part]
                 .bitcast(F32)
                 .rearrange("q (ip r u) -> q ip r u", ip=PAIRS, u=2),
                 in_=words[:].rearrange("q ip u r -> q ip r u"),
             )
 
-        def quantise_item(c):
-            xc_codes = per_item.tile([P, 2 * PAIRS * P], U32, align_bytes=64)
-            xc_scales = per_item.tile([P, 2 * PAIRS * P], U8, align_bytes=64)
+        def quantise_items(c, count):
+            pair, j = divmod(c, 2)
+            if j == 0:
+                xc_codes = xc_pairs.tile([P, 2 * ITEM_COLS], U32, align_bytes=64)
+                xc_scales = xc_pairs.tile([P, 2 * ITEM_COLS], U8, align_bytes=64)
+                xc_quantised[pair] = (xc_codes, xc_scales)
+            xc_codes, xc_scales = xc_quantised[pair]
+            cols = slice(j * ITEM_COLS, (j + count) * ITEM_COLS)
             nc.vector.quantize_mx(
-                out=xc_codes[:].bitcast(FP8X4), scales=xc_scales[:], in_=xc_grouped[c][:]
+                out=xc_codes[:, cols].bitcast(FP8X4),
+                scales=xc_scales[:, cols],
+                in_=xc_grouped[pair][:, cols.start * PACK : cols.stop * PACK],
             )
-            xc_quantised[c] = (xc_codes, xc_scales)
 
-        def filter_item(c):
-            xc_codes, xc_scales = xc_quantised[c]
-            sums[c] = psum_out.tile([P, ROWS * FEAT], F32, name="sums")
-            for ip in range(PAIRS):
+        def filter_item(c, ips):
+            pair, j = divmod(c, 2)
+            xc_codes, xc_scales = xc_quantised[pair]
+            sums[c] = psum_out.tile([P, len(ips) * 2 * FEAT], F32, name="sums")
+            for n, ip in enumerate(ips):
                 for s in range(2):
-                    node_cols = slice((s * PAIRS + ip) * P, (s * PAIRS + ip + 1) * P)
+                    first = j * ITEM_COLS + (s * PAIRS + ip) * P
+                    node_cols = slice(first, first + P)
                     w_cols = slice(s * 2 * FEAT, (s + 1) * 2 * FEAT)
                     nc.tensor.matmul_mx(
-                        out=sums[c][:, ip * 2 * FEAT : (ip + 1) * 2 * FEAT],
+                        out=sums[c][:, n * 2 * FEAT : (n + 1) * 2 * FEAT],
                         lhsT=xc_codes[:, node_cols].bitcast(FP8X4),
                         lhsT_scale=xc_scales[:, node_cols],
                         rhs=w_codes[:, w_cols].bitcast(FP8X4),
@@ -245,10 +268,12 @@ def tile_gcncheb_pb_t_kernel(tc, x, x1, x2, xt2, L, weight, bias, out):
                         stop=(s == 1),
                     )
 
-        def add_bias(c):
-            out_rows[c] = results.tile([P, ROWS * FEAT], F32, name="out_rows")
+        def add_bias(c, ips):
+            if ips[0] == 0:
+                out_rows[c] = results.tile([P, ROWS * FEAT], F32, name="out_rows")
+            cols = slice(ips[0] * 2 * FEAT, (ips[-1] + 1) * 2 * FEAT)
             nc.vector.tensor_tensor(
-                out=out_rows[c][:], in0=sums[c][:], in1=bias_rows[:], op=ALU.add
+                out=out_rows[c][:, cols], in0=sums[c][:], in1=bias_rows[:, cols], op=ALU.add
             )
 
         def add_bias_on_gpsimd(c):
@@ -263,8 +288,11 @@ def tile_gcncheb_pb_t_kernel(tc, x, x1, x2, xt2, L, weight, bias, out):
                     op=ALU.add,
                 )
 
-        def store_item(c):
-            nc.sync.dma_start(out=out[c].rearrange("(r i) o -> r (i o)", i=ROWS), in_=out_rows[c][:])
+        def store_item(c, ips=range(PAIRS)):
+            cols = slice(ips[0] * 2 * FEAT, (ips[-1] + 1) * 2 * FEAT)
+            nc.sync.dma_start(
+                out=out[c].rearrange("(r i) o -> r (i o)", i=ROWS)[:, cols], in_=out_rows[c][:, cols]
+            )
 
         turn_l(0, nc.scalar.copy)
         turn_l(1, nc.scalar.copy)
@@ -273,17 +301,16 @@ def tile_gcncheb_pb_t_kernel(tc, x, x1, x2, xt2, L, weight, bias, out):
         quantise_l(0)
         quantise_x2(0)
         quantise_l(1)
-        recurrence(0)
-        turn_item(0, 0)
         regroup_x2(2, nc.vector.tensor_copy)
         regroup_x2(3, nc.vector.tensor_copy)
-        recurrence(1)
+        recurrence(0)
+        turn_item(0, 0)
         quantise_x2(1)
+        recurrence(1)
 
         for c in range(BATCH + LAG):
             group, k = divmod(c, LOAD)
-            if (group + LOAD_AHEAD) * LOAD < BATCH:
-                load_items(order_of_need[k], (group + LOAD_AHEAD) * LOAD, LOAD)
+            load_part((group + LOAD_AHEAD) * LOAD, k)
             if c >= STORE_LAG:
                 store_item(c - STORE_LAG)
             if c % 2 == 1 and c + 3 < BATCH:
@@ -292,8 +319,10 @@ def tile_gcncheb_pb_t_kernel(tc, x, x1, x2, xt2, L, weight, bias, out):
                 if c > 0:
                     turn_item(c, 0)
                 turn_item(c, 1)
-            if 0 < c <= BATCH:
-                quantise_item(c - 1)
+            if c in (1, 2, BATCH - 1, BATCH):
+                quantise_items(c - 1, 1)
+            elif c % 2 == 0 and 2 < c < BATCH:
+                quantise_items(c - 2, 2)
             if c + REC_AHEAD < BATCH:
                 recurrence(c + REC_AHEAD)
             if c == 0:
@@ -303,12 +332,19 @@ def tile_gcncheb_pb_t_kernel(tc, x, x1, x2, xt2, L, weight, bias, out):
             if c > LAG and on_gpsimd(c - LAG - 1):
                 add_bias_on_gpsimd(c - LAG - 1)
             if c >= LAG:
-                filter_item(c - LAG)
-                if not on_gpsimd(c - LAG):
-                    add_bias(c - LAG)
+                if c - LAG == BATCH - 1:
+                    for ip in range(PAIRS):
+                        filter_item(c - LAG, [ip])
+                        add_bias(c - LAG, [ip])
+                else:
+                    filter_item(c - LAG, range(PAIRS))
+                    if not on_gpsimd(c - LAG):
+                        add_bias(c - LAG, range(PAIRS))
             if c == 0:
                 regroup_x2(4, nc.scalar.copy)
             if c + 5 < BATCH:
                 regroup_x2(c + 5, nc.scalar.copy)
-        for c in range(BATCH + LAG - STORE_LAG, BATCH):
+        for c in range(BATCH + LAG - STORE_LAG, BATCH - 1):
             store_item(c)
+        for ip in range(PAIRS):
+            store_item(BATCH - 1, [ip])

@@ -23,14 +23,13 @@ ITEM_COLS = 2 * PAIRS * P
 LOAD = 4
 LOAD_AHEAD = 3
 LOAD_BUFS = LOAD_AHEAD + 1
-REC_AHEAD = 2
-LAG = 3
-OUT_BUFS = 28
+LAG = 4
+OUT_BUFS = 24
 STORE_LAG = LAG + 2
 
 
 def on_gpsimd(c):
-    return c % 4 == 1 and c < BATCH - 3
+    return c % 4 == 1 and c < BATCH - 8
 
 
 FLOPS = 2 * BATCH * NODES * NODES * FEAT + 2 * BATCH * NODES * ORDERS * FEAT * FEAT
@@ -41,13 +40,13 @@ def tile_gcncheb_pb_t_kernel(tc, x, x1, x2, xt2, L, weight, bias, out):
     with ExitStack() as ctx:
         const = ctx.enter_context(tc.tile_pool(name="const", bufs=1))
         loads = ctx.enter_context(tc.tile_pool(name="loads", bufs=LOAD_BUFS))
-        x2_pairs = ctx.enter_context(tc.tile_pool(name="x2_pairs", bufs=3))
+        x2_pairs = ctx.enter_context(tc.tile_pool(name="x2_pairs", bufs=4))
         xc_pairs = ctx.enter_context(tc.tile_pool(name="xc_pairs", bufs=3))
-        per_item = ctx.enter_context(tc.tile_pool(name="per_item", bufs=4))
+        per_item = ctx.enter_context(tc.tile_pool(name="per_item", bufs=6))
         results = ctx.enter_context(tc.tile_pool(name="results", bufs=OUT_BUFS))
         psum_x3 = ctx.enter_context(tc.psum_pool(name="psum_x3", bufs=2))
-        psum_t = ctx.enter_context(tc.psum_pool(name="psum_t", bufs=3))
-        psum_out = ctx.enter_context(tc.psum_pool(name="psum_out", bufs=3))
+        psum_t = ctx.enter_context(tc.psum_pool(name="psum_t", bufs=4))
+        psum_out = ctx.enter_context(tc.psum_pool(name="psum_out", bufs=2))
         ctx.enter_context(tc.manual_schedule())
 
         sources = {"x": x, "x1": x1, "x2": x2, "xt2": xt2}
@@ -69,17 +68,18 @@ def tile_gcncheb_pb_t_kernel(tc, x, x1, x2, xt2, L, weight, bias, out):
             nc.sync.dma_start(
                 out=l_rows[:, pair], in_=L.rearrange("(r i) m -> r i m", i=ROWS)[:, pair]
             )
-        load_items("x2", 0, 4)
+        load_items("x2", 0, 2)
         load_items("x1", 0, 2)
         load_items("x", 0, 2)
+        load_items("x2", 2, 2)
         load_items("xt2", 0, 2)
+        load_items("x1", 2, 2)
         w_rows = const.tile([P, ORDERS, 2, FEAT], BF16)
         for h in range(2):
             nc.sync.dma_start(
                 out=w_rows[h * HALF : (h + 1) * HALF],
                 in_=weight.rearrange("j (w e) o -> w j e o", e=2),
             )
-        load_items("x1", 2, 2)
         load_items("x2", 4, 2)
         load_items("x", 2, 2)
         load_items("xt2", 2, 2)
@@ -110,19 +110,23 @@ def tile_gcncheb_pb_t_kernel(tc, x, x1, x2, xt2, L, weight, bias, out):
         ident_f32 = const.tile([P, P], F32)
         make_identity(nc, ident_f32[:])
 
+        def gpsimd_copy(out, in_):
+            nc.gpsimd.tensor_scalar(
+                out=out, in0=in_, scalar1=1.0, scalar2=0.0, op0=ALU.mult, op1=ALU.add
+            )
+
         w_grouped = const.tile([P, 2, 2, FEAT, PACK], BF16, align_bytes=64)
         nc.gpsimd.memset(w_grouped[:].rearrange("q s i o t -> q (s i o t)").bitcast(U32), 0)
         w_codes = const.tile([P, 2 * 2 * FEAT], U32, align_bytes=64)
         w_scales = const.tile([P, 2 * 2 * FEAT], U8, align_bytes=64)
 
-        def group_w():
-            for h in range(2):
-                half = slice(h * HALF, (h + 1) * HALF)
-                for s in range(2):
-                    nc.vector.tensor_copy(
-                        out=w_grouped[half, s, h].rearrange("q o (u e) -> q o u e", u=2),
-                        in_=w_rows[half, 2 * s : 2 * s + 2].rearrange("q u e o -> q o u e"),
-                    )
+        for h in range(2):
+            half = slice(h * HALF, (h + 1) * HALF)
+            for s in range(2):
+                gpsimd_copy(
+                    out=w_grouped[half, s, h].rearrange("q o (u e) -> q o u e", u=2),
+                    in_=w_rows[half, 2 * s : 2 * s + 2].rearrange("q u e o -> q o u e"),
+                )
 
         def quantise_w():
             nc.vector.quantize_mx(
@@ -156,6 +160,7 @@ def tile_gcncheb_pb_t_kernel(tc, x, x1, x2, xt2, L, weight, bias, out):
 
         x2_grouped = {}
         x2_quantised = {}
+        x3 = {}
         xt3_rows = {}
         xc_grouped = {}
         xc_quantised = {}
@@ -168,10 +173,13 @@ def tile_gcncheb_pb_t_kernel(tc, x, x1, x2, xt2, L, weight, bias, out):
                 x2_grouped[pair] = x2_pairs.tile(
                     [P, 2, FEAT, PACK], BF16, align_bytes=64, name="x2_grouped"
                 )
-            copy(
-                out=x2_grouped[pair][:, j].rearrange("p (q f) i -> p q i f", f=4),
-                in_=rows_of["x2", c].rearrange("p i (q f) -> p q i f", f=4),
-            )
+            if copy == gpsimd_copy:
+                copy(out=x2_grouped[pair][:, j], in_=rows_of["x2", c].rearrange("p i f -> p f i"))
+            else:
+                copy(
+                    out=x2_grouped[pair][:, j].rearrange("p (q f) i -> p q i f", f=4),
+                    in_=rows_of["x2", c].rearrange("p i (q f) -> p q i f", f=4),
+                )
 
         def quantise_x2(pair):
             x2_codes = x2_pairs.tile([P, 2 * FEAT], U32, align_bytes=64)
@@ -183,15 +191,15 @@ def tile_gcncheb_pb_t_kernel(tc, x, x1, x2, xt2, L, weight, bias, out):
             )
             x2_quantised[pair] = (x2_codes, x2_scales)
 
-        def recurrence(c):
+        def multiply_l(c):
             pair, j = divmod(c, 2)
             x2_codes, x2_scales = x2_quantised[pair]
             item_cols = slice(j * FEAT, (j + 1) * FEAT)
-            x3 = psum_x3.tile([P, ROWS * FEAT], F32)
+            x3[c] = psum_x3.tile([P, ROWS * FEAT], F32, name="x3")
             for i in range(ROWS):
                 node_cols = slice(i * P, (i + 1) * P)
                 nc.tensor.matmul_mx(
-                    out=x3[:, i * FEAT : (i + 1) * FEAT],
+                    out=x3[c][:, i * FEAT : (i + 1) * FEAT],
                     lhsT=l_codes[:, node_cols].bitcast(FP8X4),
                     lhsT_scale=l_scales[:, node_cols],
                     rhs=x2_codes[:, item_cols].bitcast(FP8X4),
@@ -199,10 +207,12 @@ def tile_gcncheb_pb_t_kernel(tc, x, x1, x2, xt2, L, weight, bias, out):
                     start=True,
                     stop=True,
                 )
+
+        def subtract_x1(c):
             xt3_rows[c] = per_item.tile([P, ROWS * FEAT], BF16, name="xt3_rows")
             nc.vector.scalar_tensor_tensor(
                 out=xt3_rows[c][:],
-                in0=x3[:],
+                in0=x3[c][:],
                 scalar=2.0,
                 in1=rows_of["x1", c].rearrange("r i f -> r (i f)"),
                 op0=ALU.mult,
@@ -252,7 +262,10 @@ def tile_gcncheb_pb_t_kernel(tc, x, x1, x2, xt2, L, weight, bias, out):
         def filter_item(c, ips):
             pair, j = divmod(c, 2)
             xc_codes, xc_scales = xc_quantised[pair]
-            sums[c] = psum_out.tile([P, len(ips) * 2 * FEAT], F32, name="sums")
+            if c < BATCH - 2:
+                sums[c] = psum_out.tile([P, len(ips) * 2 * FEAT], F32, name="sums")
+            else:
+                sums[c] = psum_t.tile([P, len(ips) * 2 * FEAT], F32, name="turned")
             for n, ip in enumerate(ips):
                 for s in range(2):
                     first = j * ITEM_COLS + (s * PAIRS + ip) * P
@@ -303,48 +316,83 @@ def tile_gcncheb_pb_t_kernel(tc, x, x1, x2, xt2, L, weight, bias, out):
         quantise_l(1)
         regroup_x2(2, nc.vector.tensor_copy)
         regroup_x2(3, nc.vector.tensor_copy)
-        recurrence(0)
+        multiply_l(0)
+        subtract_x1(0)
         turn_item(0, 0)
         quantise_x2(1)
-        recurrence(1)
+        multiply_l(1)
+        subtract_x1(1)
+        turn_item(0, 1)
+        for n in (2, 3):
+            multiply_l(n)
+            subtract_x1(n)
 
-        for c in range(BATCH + LAG):
+        def move_data(c):
             group, k = divmod(c, LOAD)
             load_part((group + LOAD_AHEAD) * LOAD, k)
-            if c >= STORE_LAG:
+            if 0 <= c - STORE_LAG < BATCH - 1:
                 store_item(c - STORE_LAG)
-            if c % 2 == 1 and c + 3 < BATCH:
-                quantise_x2((c + 3) // 2)
+
+        def regroup_ahead(c):
+            if c < 2:
+                ahead = (2 * c + 4, 2 * c + 5)
+            else:
+                ahead = (c + 6,)
+            for item in ahead:
+                if item < BATCH:
+                    on_pool = item % 4 == 2 and item >= 8
+                    regroup_x2(item, gpsimd_copy if on_pool else nc.scalar.copy)
+
+        for c in range(0, BATCH + STORE_LAG, 2):
+            move_data(c)
+            if c == 2:
+                quantise_x2(2)
+                quantise_x2(3)
+            elif 2 < c < BATCH - LAG:
+                quantise_x2(c // 2 + 2)
             if c < BATCH:
                 if c > 0:
                     turn_item(c, 0)
-                turn_item(c, 1)
-            if c in (1, 2, BATCH - 1, BATCH):
-                quantise_items(c - 1, 1)
-            elif c % 2 == 0 and 2 < c < BATCH:
-                quantise_items(c - 2, 2)
-            if c + REC_AHEAD < BATCH:
-                recurrence(c + REC_AHEAD)
-            if c == 0:
-                group_w()
-            if c == 1:
-                quantise_w()
+                    turn_item(c, 1)
             if c > LAG and on_gpsimd(c - LAG - 1):
                 add_bias_on_gpsimd(c - LAG - 1)
-            if c >= LAG:
-                if c - LAG == BATCH - 1:
-                    for ip in range(PAIRS):
-                        filter_item(c - LAG, [ip])
-                        add_bias(c - LAG, [ip])
-                else:
-                    filter_item(c - LAG, range(PAIRS))
-                    if not on_gpsimd(c - LAG):
-                        add_bias(c - LAG, range(PAIRS))
+            regroup_ahead(c)
+            if c == BATCH:
+                quantise_items(c - 2, 1)
+                quantise_items(c - 1, 1)
+            elif 0 < c < BATCH:
+                quantise_items(c - 2, 2)
+            if c < BATCH:
+                turn_item(c + 1, 0)
+                turn_item(c + 1, 1)
             if c == 0:
-                regroup_x2(4, nc.scalar.copy)
-            if c + 5 < BATCH:
-                regroup_x2(c + 5, nc.scalar.copy)
-        for c in range(BATCH + LAG - STORE_LAG, BATCH - 1):
-            store_item(c)
+                ahead = []
+            elif c == 2:
+                ahead = [4, 5, 6]
+            else:
+                ahead = [n for n in (c + 3, c + 4) if n < BATCH]
+            behind = [n for n in (c - LAG, c - LAG + 1) if 0 <= n < BATCH]
+            whole = [n for n in behind if n < BATCH - 1]
+            for n in ahead[:2]:
+                multiply_l(n)
+            for n in whole:
+                filter_item(n, range(PAIRS))
+            for j in range(2):
+                if j < len(ahead):
+                    subtract_x1(ahead[j])
+                if j < len(whole) and not on_gpsimd(whole[j]):
+                    add_bias(whole[j], range(PAIRS))
+            for n in ahead[2:]:
+                multiply_l(n)
+                subtract_x1(n)
+            if c == 2:
+                quantise_w()
+            if BATCH - 1 in behind:
+                for ip in range(PAIRS):
+                    filter_item(BATCH - 1, [ip])
+                    add_bias(BATCH - 1, [ip])
+            move_data(c + 1)
+            if c < BATCH:
+                regroup_ahead(c + 1)
         for ip in range(PAIRS):
             store_item(BATCH - 1, [ip])

from contextlib import ExitStack

import concourse.mybir as mybir
from concourse.masks import make_identity

BF16 = mybir.dt.bfloat16
F32 = mybir.dt.float32
U32 = mybir.dt.uint32
U8 = mybir.dt.uint8
FP8X4 = mybir.dt.float8_e4m3fn_x4
ALU = mybir.AluOpType

P = 128
HALF = P // 2
PACK = 4
BATCH = 32
NODES = 512
FEAT = 128
ORDERS = 4
ROWS = NODES // P
PAIRS = ROWS // 2
ITEM_COLS = 2 * PAIRS * P
LOAD = 4
LOAD_AHEAD = 3
LOAD_BUFS = LOAD_AHEAD + 1
LAG = 4
OUT_BUFS = 24
STORE_LAG = LAG + 2


def on_gpsimd(c):
    return c % 4 == 1 and c < BATCH - 8


FLOPS = 2 * BATCH * NODES * NODES * FEAT + 2 * BATCH * NODES * ORDERS * FEAT * FEAT


def tile_gcncheb_pb_t_kernel(tc, x, x1, x2, xt2, L, weight, bias, out):
    nc = tc.nc
    with ExitStack() as ctx:
        const = ctx.enter_context(tc.tile_pool(name="const", bufs=1))
        loads = ctx.enter_context(tc.tile_pool(name="loads", bufs=LOAD_BUFS))
        x2_pairs = ctx.enter_context(tc.tile_pool(name="x2_pairs", bufs=4))
        xc_pairs = ctx.enter_context(tc.tile_pool(name="xc_pairs", bufs=3))
        per_item = ctx.enter_context(tc.tile_pool(name="per_item", bufs=6))
        results = ctx.enter_context(tc.tile_pool(name="results", bufs=OUT_BUFS))
        psum_x3 = ctx.enter_context(tc.psum_pool(name="psum_x3", bufs=2))
        psum_t = ctx.enter_context(tc.psum_pool(name="psum_t", bufs=4))
        psum_out = ctx.enter_context(tc.psum_pool(name="psum_out", bufs=2))
        ctx.enter_context(tc.manual_schedule())

        sources = {"x": x, "x1": x1, "x2": x2, "xt2": xt2}
        rows_of = {}

        def load_items(name, first, count):
            pool, tag = (loads, name) if count == LOAD and first > 0 else (const, f"{name}_{first}")
            rows = pool.tile([P, count, ROWS, FEAT], BF16, name=tag)
            nc.sync.dma_start(
                out=rows[:],
                in_=sources[name][first : first + count].rearrange("c (r i) f -> r c i f", i=ROWS),
            )
            for j in range(count):
                rows_of[name, first + j] = rows[:, j]

        l_rows = const.tile([P, ROWS, NODES], BF16)
        for ip in range(PAIRS):
            pair = slice(2 * ip, 2 * ip + 2)
            nc.sync.dma_start(
                out=l_rows[:, pair], in_=L.rearrange("(r i) m -> r i m", i=ROWS)[:, pair]
            )
        load_items("x2", 0, 2)
        load_items("x1", 0, 2)
        load_items("x", 0, 2)
        load_items("x2", 2, 2)
        load_items("xt2", 0, 2)
        load_items("x1", 2, 2)
        w_rows = const.tile([P, ORDERS, 2, FEAT], BF16)
        for h in range(2):
            nc.sync.dma_start(
                out=w_rows[h * HALF : (h + 1) * HALF],
                in_=weight.rearrange("j (w e) o -> w j e o", e=2),
            )
        load_items("x2", 4, 2)
        load_items("x", 2, 2)
        load_items("xt2", 2, 2)
        load_items("x2", 6, 2)
        load_items("x1", 4, 2)
        bias_rows = const.tile([P, ROWS * FEAT], BF16)
        nc.sync.dma_start(out=bias_rows[:], in_=bias[0].rearrange("(r i) o -> r (i o)", i=ROWS))
        load_items("x2", 8, 2)
        load_items("x", 4, 2)
        load_items("xt2", 4, 2)
        load_items("x1", 6, 2)
        load_items("x2", 10, 2)
        load_items("x", 6, 2)
        load_items("xt2", 6, 2)

        def load_part(first, k):
            name = ("x1", "x2", "x", "xt2")[k]
            if name == "x2":
                first += LOAD
            if first < BATCH:
                load_items(name, first, LOAD)

        for k in range(4):
            load_part(2 * LOAD, k)

        ident_bf16 = const.tile([P, P], BF16)
        make_identity(nc, ident_bf16[:])
        ident_f32 = const.tile([P, P], F32)
        make_identity(nc, ident_f32[:])

        def gpsimd_copy(out, in_):
            nc.gpsimd.tensor_scalar(
                out=out, in0=in_, scalar1=1.0, scalar2=0.0, op0=ALU.mult, op1=ALU.add
            )

        w_grouped = const.tile([P, 2, 2, FEAT, PACK], BF16, align_bytes=64)
        nc.gpsimd.memset(w_grouped[:].rearrange("q s i o t -> q (s i o t)").bitcast(U32), 0)
        w_codes = const.tile([P, 2 * 2 * FEAT], U32, align_bytes=64)
        w_scales = const.tile([P, 2 * 2 * FEAT], U8, align_bytes=64)

        for h in range(2):
            half = slice(h * HALF, (h + 1) * HALF)
            for s in range(2):
                gpsimd_copy(
                    out=w_grouped[half, s, h].rearrange("q o (u e) -> q o u e", u=2),
                    in_=w_rows[half, 2 * s : 2 * s + 2].rearrange("q u e o -> q o u e"),
                )

        def quantise_w():
            nc.vector.quantize_mx(
                out=w_codes[:].bitcast(FP8X4),
                scales=w_scales[:],
                in_=w_grouped[:].rearrange("q s i o t -> q (s i o t)"),
            )

        l_grouped = const.tile([P, ROWS, P, PACK], BF16, align_bytes=64)
        l_codes = const.tile([P, ROWS * P], U32, align_bytes=64)
        l_scales = const.tile([P, ROWS * P], U8, align_bytes=64)

        def turn_l(ip, copy):
            l_planes = psum_t.tile([P, 2, PACK, P], BF16, name="turned")
            for i2 in range(2):
                l_cols = l_rows[:, 2 * ip + i2, :].rearrange("r (p t) -> r p t", t=PACK)
                for t in range(PACK):
                    nc.tensor.transpose(l_planes[:, i2, t, :], l_cols[:, :, t], ident_bf16[:])
            copy(
                out=l_grouped[:, 2 * ip : 2 * ip + 2],
                in_=l_planes[:].rearrange("p i t r -> p i r t"),
            )

        def quantise_l(ip):
            cols = slice(2 * ip * P, 2 * (ip + 1) * P)
            nc.vector.quantize_mx(
                out=l_codes[:, cols].bitcast(FP8X4),
                scales=l_scales[:, cols],
                in_=l_grouped[:, 2 * ip : 2 * ip + 2].rearrange("p i r t -> p (i r t)"),
            )

        x2_grouped = {}
        x2_quantised = {}
        x3 = {}
        xt3_rows = {}
        xc_grouped = {}
        xc_quantised = {}
        sums = {}
        out_rows = {}

        def regroup_x2(c, copy):
            pair, j = divmod(c, 2)
            if j == 0:
                x2_grouped[pair] = x2_pairs.tile(
                    [P, 2, FEAT, PACK], BF16, align_bytes=64, name="x2_grouped"
                )
            if copy == gpsimd_copy:
                copy(out=x2_grouped[pair][:, j], in_=rows_of["x2", c].rearrange("p i f -> p f i"))
            else:
                copy(
                    out=x2_grouped[pair][:, j].rearrange("p (q f) i -> p q i f", f=4),
                    in_=rows_of["x2", c].rearrange("p i (q f) -> p q i f", f=4),
                )

        def quantise_x2(pair):
            x2_codes = x2_pairs.tile([P, 2 * FEAT], U32, align_bytes=64)
            x2_scales = x2_pairs.tile([P, 2 * FEAT], U8, align_bytes=64)
            nc.vector.quantize_mx(
                out=x2_codes[:].bitcast(FP8X4),
                scales=x2_scales[:],
                in_=x2_grouped[pair][:].rearrange("p c f t -> p (c f t)"),
            )
            x2_quantised[pair] = (x2_codes, x2_scales)

        def multiply_l(c):
            pair, j = divmod(c, 2)
            x2_codes, x2_scales = x2_quantised[pair]
            item_cols = slice(j * FEAT, (j + 1) * FEAT)
            x3[c] = psum_x3.tile([P, ROWS * FEAT], F32, name="x3")
            for i in range(ROWS):
                node_cols = slice(i * P, (i + 1) * P)
                nc.tensor.matmul_mx(
                    out=x3[c][:, i * FEAT : (i + 1) * FEAT],
                    lhsT=l_codes[:, node_cols].bitcast(FP8X4),
                    lhsT_scale=l_scales[:, node_cols],
                    rhs=x2_codes[:, item_cols].bitcast(FP8X4),
                    rhs_scale=x2_scales[:, item_cols],
                    start=True,
                    stop=True,
                )

        def subtract_x1(c):
            xt3_rows[c] = per_item.tile([P, ROWS * FEAT], BF16, name="xt3_rows")
            nc.vector.scalar_tensor_tensor(
                out=xt3_rows[c][:],
                in0=x3[c][:],
                scalar=2.0,
                in1=rows_of["x1", c].rearrange("r i f -> r (i f)"),
                op0=ALU.mult,
                op1=ALU.subtract,
            )

        def turn_item(c, s):
            if s == 0:
                if c % 2 == 0:
                    xc_grouped[c // 2] = xc_pairs.tile(
                        [P, 2 * ITEM_COLS * PACK], BF16, align_bytes=64, name="xc_grouped"
                    )
                pair = [rows_of[name, c].rearrange("r i f -> r (i f)") for name in ("x", "x1")]
            else:
                pair = [rows_of["xt2", c].rearrange("r i f -> r (i f)"), xt3_rows[c][:]]
            part = ITEM_COLS * PACK // 2
            start = (c % 2 * 2 + s) * part
            words = psum_t.tile([P, PAIRS, 2, P], F32, name="turned")
            for ip in range(PAIRS):
                for u in range(2):
                    nc.tensor.transpose(
                        words[:, ip, u, :],
                        pair[u].bitcast(F32)[:, ip * P : (ip + 1) * P],
                        ident_f32[:],
                    )
            nc.scalar.copy(
                out=xc_grouped[c // 2][:, start : start + part]
                .bitcast(F32)
                .rearrange("q (ip r u) -> q ip r u", ip=PAIRS, u=2),
                in_=words[:].rearrange("q ip u r -> q ip r u"),
            )

        def quantise_items(c, count):
            pair, j = divmod(c, 2)
            if j == 0:
                xc_codes = xc_pairs.tile([P, 2 * ITEM_COLS], U32, align_bytes=64)
                xc_scales = xc_pairs.tile([P, 2 * ITEM_COLS], U8, align_bytes=64)
                xc_quantised[pair] = (xc_codes, xc_scales)
            xc_codes, xc_scales = xc_quantised[pair]
            cols = slice(j * ITEM_COLS, (j + count) * ITEM_COLS)
            nc.vector.quantize_mx(
                out=xc_codes[:, cols].bitcast(FP8X4),
                scales=xc_scales[:, cols],
                in_=xc_grouped[pair][:, cols.start * PACK : cols.stop * PACK],
            )

        def filter_item(c, ips):
            pair, j = divmod(c, 2)
            xc_codes, xc_scales = xc_quantised[pair]
            if c < BATCH - 2:
                sums[c] = psum_out.tile([P, len(ips) * 2 * FEAT], F32, name="sums")
            else:
                sums[c] = psum_t.tile([P, len(ips) * 2 * FEAT], F32, name="turned")
            for n, ip in enumerate(ips):
                for s in range(2):
                    first = j * ITEM_COLS + (s * PAIRS + ip) * P
                    node_cols = slice(first, first + P)
                    w_cols = slice(s * 2 * FEAT, (s + 1) * 2 * FEAT)
                    nc.tensor.matmul_mx(
                        out=sums[c][:, n * 2 * FEAT : (n + 1) * 2 * FEAT],
                        lhsT=xc_codes[:, node_cols].bitcast(FP8X4),
                        lhsT_scale=xc_scales[:, node_cols],
                        rhs=w_codes[:, w_cols].bitcast(FP8X4),
                        rhs_scale=w_scales[:, w_cols],
                        start=(s == 0),
                        stop=(s == 1),
                    )

        def add_bias(c, ips):
            if ips[0] == 0:
                out_rows[c] = results.tile([P, ROWS * FEAT], F32, name="out_rows")
            cols = slice(ips[0] * 2 * FEAT, (ips[-1] + 1) * 2 * FEAT)
            nc.vector.tensor_tensor(
                out=out_rows[c][:, cols], in0=sums[c][:], in1=bias_rows[:, cols], op=ALU.add
            )

        def add_bias_on_gpsimd(c):
            out_rows[c] = results.tile([P, ROWS * FEAT], F32, name="out_rows")
            nc.scalar.copy(out=out_rows[c][:], in_=sums[c][:])
            for h in range(2):
                cols = slice(h * ROWS * FEAT // 2, (h + 1) * ROWS * FEAT // 2)
                nc.gpsimd.tensor_tensor(
                    out=out_rows[c][:, cols],
                    in0=out_rows[c][:, cols],
                    in1=bias_rows[:, cols],
                    op=ALU.add,
                )

        def store_item(c, ips=range(PAIRS)):
            cols = slice(ips[0] * 2 * FEAT, (ips[-1] + 1) * 2 * FEAT)
            nc.sync.dma_start(
                out=out[c].rearrange("(r i) o -> r (i o)", i=ROWS)[:, cols], in_=out_rows[c][:, cols]
            )

        turn_l(0, nc.scalar.copy)
        turn_l(1, nc.scalar.copy)
        regroup_x2(0, nc.vector.tensor_copy)
        regroup_x2(1, nc.vector.tensor_copy)
        quantise_l(0)
        quantise_x2(0)
        quantise_l(1)
        regroup_x2(2, nc.vector.tensor_copy)
        regroup_x2(3, nc.vector.tensor_copy)
        multiply_l(0)
        subtract_x1(0)
        turn_item(0, 0)
        quantise_x2(1)
        multiply_l(1)
        subtract_x1(1)
        turn_item(0, 1)
        for n in (2, 3):
            multiply_l(n)
            subtract_x1(n)

        def move_data(c):
            group, k = divmod(c, LOAD)
            load_part((group + LOAD_AHEAD) * LOAD, k)
            if 0 <= c - STORE_LAG < BATCH - 1:
                store_item(c - STORE_LAG)

        def regroup_ahead(c):
            if c < 2:
                ahead = (2 * c + 4, 2 * c + 5)
            else:
                ahead = (c + 6,)
            for item in ahead:
                if item < BATCH:
                    on_pool = item % 4 == 2 and item >= 8
                    regroup_x2(item, gpsimd_copy if on_pool else nc.scalar.copy)

        for c in range(0, BATCH + STORE_LAG, 2):
            move_data(c)
            if c == 2:
                quantise_x2(2)
                quantise_x2(3)
            elif 2 < c < BATCH - LAG:
                quantise_x2(c // 2 + 2)
            if c < BATCH:
                if c > 0:
                    turn_item(c, 0)
                    turn_item(c, 1)
            if c > LAG and on_gpsimd(c - LAG - 1):
                add_bias_on_gpsimd(c - LAG - 1)
            regroup_ahead(c)
            if c == BATCH:
                quantise_items(c - 2, 1)
                quantise_items(c - 1, 1)
            elif 0 < c < BATCH:
                quantise_items(c - 2, 2)
            if c < BATCH:
                turn_item(c + 1, 0)
                turn_item(c + 1, 1)
            if c == 0:
                ahead = []
            elif c == 2:
                ahead = [4, 5, 6]
            else:
                ahead = [n for n in (c + 3, c + 4) if n < BATCH]
            behind = [n for n in (c - LAG, c - LAG + 1) if 0 <= n < BATCH]
            whole = [n for n in behind if n < BATCH - 1]
            for n in ahead[:2]:
                multiply_l(n)
            for n in whole:
                filter_item(n, range(PAIRS))
            for j in range(2):
                if j < len(ahead):
                    subtract_x1(ahead[j])
                if j < len(whole) and not on_gpsimd(whole[j]):
                    add_bias(whole[j], range(PAIRS))
            for n in ahead[2:]:
                multiply_l(n)
                subtract_x1(n)
            if c == 2:
                quantise_w()
            if BATCH - 1 in behind:
                for ip in range(PAIRS):
                    filter_item(BATCH - 1, [ip])
                    add_bias(BATCH - 1, [ip])
            move_data(c + 1)
            if c < BATCH:
                regroup_ahead(c + 1)
        for ip in range(PAIRS):
            store_item(BATCH - 1, [ip])
